import numpy as np
import ml_dtypes


def mxq(x, axis, fmt="e4m3"):
    dtype, down = {"e4m3": (ml_dtypes.float8_e4m3fn, 7), "e5m2": (ml_dtypes.float8_e5m2, 14)}[fmt]
    v = np.moveaxis(np.asarray(x, np.float32).astype(ml_dtypes.bfloat16).astype(np.float64), axis, -1)
    blocks = v.reshape(v.shape[:-1] + (-1, 32))
    amax = np.abs(blocks).max(-1, keepdims=True)
    byte = np.maximum(np.where(amax > 0, np.frexp(amax)[1] - 1 + 127, 0) - down, 1)
    scale = np.exp2(byte - 127.0)
    codes = (blocks / scale).astype(np.float32).astype(dtype).astype(np.float64)
    return np.moveaxis((codes * scale).reshape(v.shape), -1, axis)


WIDE = False


def mx_kscale(k):
    if not WIDE:
        return np.ones(k)
    levels = np.array([10, -10, 5, -5, 0])
    a = np.random.permutation(np.resize(levels, k // 512 * 4)).reshape(k // 512, 4)
    idx = np.arange(k)
    return np.exp2(a[idx // 512, idx % 128 // 32])


BF16 = ml_dtypes.bfloat16


def bf(x):
    return np.asarray(x, np.float32).astype(BF16)


def f64(x):
    return np.asarray(x).astype(np.float64)


B, NB, DIM, R = 2048, 2, 1024, 2
INTER = DIM // R
EPS = 1e-5


def sigmoid(v):
    return 1.0 / (1.0 + np.exp(-v))


def setup_inputs():
    u = mx_kscale(INTER)
    return {
        "t": bf(np.random.standard_normal((B, NB, DIM))),
        "W1": bf(np.random.standard_normal((NB, INTER, DIM)) / np.sqrt(NB * DIM)),
        "b1": bf(0.3 * np.random.standard_normal((NB, INTER))),
        "g1": bf((1.0 + 0.2 * np.random.standard_normal((NB, INTER))) * u),
        "beta1": bf(0.3 * np.random.standard_normal((NB, INTER)) * u),
        "m1": bf(0.3 * np.random.standard_normal((NB, INTER))),
        "v1": bf(np.random.uniform(0.5, 1.5, (NB, INTER))),
        "W2": bf(np.random.standard_normal((NB, DIM, INTER)) * 1.5 / np.sqrt(INTER) / u),
        "b2": bf(0.3 * np.random.standard_normal((NB, DIM))),
        "g2": bf(1.0 + 0.2 * np.random.standard_normal((NB, DIM))),
        "beta2": bf(0.3 * np.random.standard_normal((NB, DIM))),
        "m2": bf(0.3 * np.random.standard_normal((NB, DIM))),
        "v2": bf(np.random.uniform(0.5, 1.5, (NB, DIM))),
    }


def reference(t, W1, b1, g1, beta1, m1, v1, W2, b2, g2, beta2, m2, v2):
    t = f64(t)
    s = t.sum(axis=1)
    a = mxq(s, 1, "e4m3") @ mxq(f64(W1), 2, "e4m3").transpose(0, 2, 1)
    h = a.transpose(1, 0, 2) + f64(b1)
    h = (h - f64(m1)) * (1.0 / np.sqrt(f64(v1) + EPS)) * f64(g1) + f64(beta1)
    h = np.maximum(h, 0.0)
    c = mxq(h, 2, "e4m3").transpose(1, 0, 2) @ mxq(f64(W2), 2, "e4m3").transpose(0, 2, 1)
    y = c.transpose(1, 0, 2) + f64(b2)
    y = (y - f64(m2)) * (1.0 / np.sqrt(f64(v2) + EPS)) * f64(g2) + f64(beta2)
    w = sigmoid(y)
    return (w * t).sum(axis=1) * 3.0

@@ -1,0 +1,374 @@
+from contextlib import ExitStack
+
+import concourse.mybir as mybir
+from concourse.masks import make_identity
+
+F32 = mybir.dt.float32
+BF16 = mybir.dt.bfloat16
+U32 = mybir.dt.uint32
+U8 = mybir.dt.uint8
+FP8X4 = mybir.dt.float8_e4m3fn_x4
+ALU = mybir.AluOpType
+ACT = mybir.ActivationFunctionType
+
+P = 128
+B, NB, DIM, INTER = 2048, 2, 1024, 512
+EPS = 1e-5
+CH = 512
+NCH = B // CH
+BT = CH // P
+FLOPS = 2 * B * DIM * NB * INTER * 2
+
+
+def tile_af_2_pa_t_kernel(tc, t, W1, b1, g1, beta1, m1, v1, W2, b2, g2, beta2, m2, v2, out):
+    nc = tc.nc
+    with ExitStack() as ctx:
+        ctx.enter_context(tc.manual_schedule())
+        const = ctx.enter_context(tc.tile_pool(name="const", bufs=1))
+        bigp = ctx.enter_context(tc.tile_pool(name="bigp", bufs=3))
+        wgrpp = ctx.enter_context(tc.tile_pool(name="wgrpp", bufs=4))
+        t1p = ctx.enter_context(tc.tile_pool(name="t1p", bufs=4))
+        sgp = ctx.enter_context(tc.tile_pool(name="sgp", bufs=2))
+        swp = ctx.enter_context(tc.tile_pool(name="swp", bufs=2))
+        hp = ctx.enter_context(tc.tile_pool(name="hp", bufs=2))
+        wtp = ctx.enter_context(tc.tile_pool(name="wtp", bufs=12))
+        op = ctx.enter_context(tc.tile_pool(name="op", bufs=2))
+        tp = ctx.enter_context(tc.psum_pool(name="tp", bufs=4))
+        mp = ctx.enter_context(tc.psum_pool(name="mp", bufs=4))
+
+        t_v = t.rearrange("(p k) n d -> p k n d", k=NCH * BT)
+        out_v = out.rearrange("(p k) d -> p k d", k=NCH * BT)
+
+        ident = const.tile([P, P], F32, name="ident")
+        w1w = const.tile([P, 2, NB * INTER], U32, name="w1w", align_bytes=64)
+        w1s = const.tile([P, 2, NB * INTER], U8, name="w1s", align_bytes=64)
+        w2w = const.tile([P, NB, DIM], U32, name="w2w", align_bytes=64)
+        w2s = const.tile([P, NB, DIM], U8, name="w2s", align_bytes=64)
+        t_sb = [const.tile([P, BT, NB, DIM], BF16, name="t_sb%d" % c) for c in range(NCH)]
+        x1 = const.tile([P, 256], BF16, name="x1")
+        x2 = const.tile([P, P], BF16, name="x2")
+        xf1 = const.tile([P, 2, P], F32, name="xf1")
+        xf2 = const.tile([P, P], F32, name="xf2")
+        pr = [const.tile([P, 5, 8], F32, name="pr1"), const.tile([P, 5, 16], F32, name="pr2")]
+        sc = [const.tile([P, 8], F32, name="sc1"), const.tile([P, 16], F32, name="sc2")]
+        bi = [const.tile([P, 8], F32, name="bi1"), const.tile([P, 16], F32, name="bi2")]
+        rs = [const.tile([P, 8], F32, name="rs1"), const.tile([P, 16], F32, name="rs2")]
+        df = [const.tile([P, 8], F32, name="df1"), const.tile([P, 16], F32, name="df2")]
+
+        live = {}
+
+        def load_t(c, pieces):
+            step = BT // pieces
+            for i in range(pieces):
+                nc.sync.dma_start(out=t_sb[c][:, i * step:(i + 1) * step], in_=t_v[:, c * BT + i * step:c * BT + (i + 1) * step])
+
+        def load_w1(n):
+            raw = bigp.tile([P, 4096], BF16, name="wraw", tag="big")
+            nc.sync.dma_start(out=raw.rearrange("p (u x) -> p u x", u=2), in_=W1[n].rearrange("(u p e) d -> p u (e d)", u=2, p=P, e=2))
+            live[("w1raw", n)] = raw
+
+        def load_w2(n):
+            raw = bigp.tile([P, 4096], BF16, name="wraw", tag="big")
+            nc.sync.dma_start(out=raw.rearrange("p (k i) -> p k i", k=8), in_=W2[n].rearrange("(k p) i -> p k i", p=P))
+            live[("w2raw", n)] = raw
+
+        def load_params(stage):
+            if stage == 0:
+                for v, vec in enumerate((b1, g1, beta1, m1, v1)):
+                    nc.scalar.dma_start(out=x1[4 * v:4 * v + 4, :], in_=vec.rearrange("n (u c) -> (n u) c", c=256))
+            else:
+                for v, vec in enumerate((b2, g2, beta2, m2, v2)):
+                    nc.scalar.dma_start(out=x2[16 * v:16 * v + 16, :], in_=vec.rearrange("n (k c) -> (n k) c", c=P))
+
+        def params_cast(stage):
+            if stage == 0:
+                nc.vector.tensor_copy(out=xf1[:], in_=x1.rearrange("r (p e) -> r e p", e=2))
+            else:
+                nc.vector.tensor_copy(out=xf2[:], in_=x2[:])
+
+        def params_pe(stage):
+            if stage == 0:
+                bank = tp.tile([P, 2, P], F32, name="tpb", tag="tp")
+                for e in range(2):
+                    nc.tensor.transpose(bank[:, e, :], xf1[:, e, :], ident[:])
+                nc.vector.tensor_copy(out=pr[0].rearrange("p v (e j) -> p v e j", e=2), in_=bank[:, :, 0:20].rearrange("p e (v j) -> p v e j", v=5))
+            else:
+                bank = tp.tile([P, P], F32, name="tpb", tag="tp")
+                nc.tensor.transpose(bank[:], xf2[:], ident[:])
+                nc.vector.tensor_copy(out=pr[1][:], in_=bank[:, 0:80].rearrange("p (v j) -> p v j", v=5))
+            q = pr[stage]
+            nc.vector.tensor_scalar_add(out=rs[stage][:], in0=q[:, 4, :], scalar1=EPS)
+            nc.scalar.sqrt(out=rs[stage][:], in_=rs[stage][:])
+            nc.vector.reciprocal(out=rs[stage][:], in_=rs[stage][:])
+            nc.vector.tensor_tensor(out=sc[stage][:], in0=q[:, 1, :], in1=rs[stage][:], op=ALU.mult)
+            nc.vector.tensor_tensor(out=df[stage][:], in0=q[:, 0, :], in1=q[:, 3, :], op=ALU.subtract)
+            nc.vector.tensor_tensor(out=df[stage][:], in0=df[stage][:], in1=sc[stage][:], op=ALU.mult)
+            nc.vector.tensor_tensor(out=bi[stage][:], in0=df[stage][:], in1=q[:, 2, :], op=ALU.add)
+
+        def evac(eng, dst, src):
+            if eng == "S":
+                nc.scalar.copy(out=dst, in_=src)
+            else:
+                nc.vector.tensor_copy(out=dst, in_=src)
+
+        def w_bank(kind, n, a, b):
+            bank = tp.tile([P, 2, 256], F32, name="tpb", tag="tp")
+            for x in range(2):
+                if kind == 1:
+                    words = live[("w1raw", n)][:, b * 2048 + x * 1024:b * 2048 + (x + 1) * 1024].bitcast(F32)[:, 256 * a:256 * a + 256]
+                else:
+                    k = 4 * a + 2 * b + x
+                    words = live[("w2raw", n)][:, k * 512:(k + 1) * 512].bitcast(F32)
+                for u in range(2):
+                    nc.tensor.transpose(bank[:, u, x * P:(x + 1) * P], words[:, u * P:(u + 1) * P], ident[:])
+            live[("wbank", kind, n, a, b)] = bank
+
+        def w_evac(kind, n, a, b, eng):
+            if b == 0:
+                live[("wgrp", kind, n, a)] = wgrpp.tile([P, 2048], BF16, name="wgrp", align_bytes=64)
+            dst = live[("wgrp", kind, n, a)].bitcast(F32).rearrange("p (c u) -> p c u", u=2)[:, b * 256:(b + 1) * 256, :]
+            evac(eng, dst, live[("wbank", kind, n, a, b)].rearrange("p u c -> p c u"))
+
+        def w_quant(kind, n, a):
+            grp = live[("wgrp", kind, n, a)]
+            if kind == 1:
+                cols = slice(n * 512, (n + 1) * 512)
+                nc.vector.quantize_mx(out=w1w[:, a, cols].bitcast(FP8X4), scales=w1s[:, a, cols], in_=grp[:])
+            else:
+                cols = slice(a * 512, (a + 1) * 512)
+                nc.vector.quantize_mx(out=w2w[:, n, cols].bitcast(FP8X4), scales=w2s[:, n, cols], in_=grp[:])
+
+        def t1_bank(c, g, half, n):
+            bank = tp.tile([P, 2, 256], F32, name="tpb", tag="tp")
+            for x in range(2):
+                words = t_sb[c][:, 2 * half + x, n, :].bitcast(F32)
+                for u in range(2):
+                    nc.tensor.transpose(bank[:, u, x * P:(x + 1) * P], words[:, 256 * g + u * P:256 * g + (u + 1) * P], ident[:])
+            live[("tbank", c, g, half, n)] = bank
+
+        def e1(c, g, half):
+            t1T = t1p.tile([P, 256, 2], F32, name="t1T")
+            nc.scalar.copy(out=t1T[:], in_=live[("tbank", c, g, half, 1)].rearrange("p u b -> p b u"))
+            live[("t1T", c, g, half)] = t1T
+
+        def s_add(c, g, half):
+            if ("sg", c, g) not in live:
+                live[("sg", c, g)] = sgp.tile([P, 2048], BF16, name="sg", align_bytes=64)
+            dst = live[("sg", c, g)][:, half * 1024:(half + 1) * 1024].rearrange("p (b u e) -> p b u e", u=2, e=2)
+            in0 = live[("tbank", c, g, half, 0)].rearrange("p u b -> p (u b)").bitcast(BF16).rearrange("p (u b e) -> p b u e", u=2, e=2)
+            in1 = live[("t1T", c, g, half)].rearrange("p b u -> p (b u)").bitcast(BF16).rearrange("p (b u e) -> p b u e", u=2, e=2)
+            nc.vector.tensor_tensor(out=dst, in0=in0, in1=in1, op=ALU.add)
+
+        def q1(c, g):
+            if ("sw", c) not in live:
+                live[("sw", c)] = swp.tile([P, 2, CH], U32, name="sw", align_bytes=64)
+                live[("ss", c)] = swp.tile([P, 2, CH], U8, name="ss", align_bytes=64)
+            nc.vector.quantize_mx(out=live[("sw", c)][:, g, :].bitcast(FP8X4), scales=live[("ss", c)][:, g, :], in_=live[("sg", c, g)][:])
+
+        def mm1(c, n):
+            for tt in range(4):
+                acc = mp.tile([P, CH], F32, name="acc", tag="mp")
+                cols = slice(n * 512 + tt * P, n * 512 + (tt + 1) * P)
+                for g in range(2):
+                    nc.tensor.matmul_mx(out=acc[:], lhsT=w1w[:, g, cols].bitcast(FP8X4), lhsT_scale=w1s[:, g, cols],
+                                        rhs=live[("sw", c)][:, g, :].bitcast(FP8X4), rhs_scale=live[("ss", c)][:, g, :],
+                                        start=(g == 0), stop=(g == 1))
+                live[("acc1", c, n, tt)] = acc
+
+        def relu(c, n):
+            hT = hp.tile([P, 4, CH], BF16, name="hT")
+            for tt in range(4):
+                col = (tt % 2) * 4 + 2 * n + tt // 2
+                nc.scalar.activation(out=hT[:, tt, :], in_=live[("acc1", c, n, tt)][:], func=ACT.Relu,
+                                     bias=bi[0][:, col:col + 1], scale=sc[0][:, col:col + 1])
+            live[("hT", c, n)] = hT
+
+        def rg(c, n, eng="V"):
+            hg = hp.tile([P, 4 * CH], BF16, name="hg", align_bytes=64)
+            dst = hg.rearrange("p (c i t) -> p c t i", i=4, t=4)
+            src = live[("hT", c, n)].rearrange("p t (c i) -> p c t i", i=4)
+            if eng == "V":
+                nc.vector.tensor_copy(out=dst, in_=src)
+            elif eng == "G":
+                nc.gpsimd.tensor_scalar(out=dst, in0=src, scalar1=1.0, scalar2=0.0, op0=ALU.mult, op1=ALU.add)
+            else:
+                nc.scalar.copy(out=dst, in_=src)
+            live[("hg", c, n)] = hg
+
+        def q2(c, n):
+            hw = hp.tile([P, CH], U32, name="hw", align_bytes=64)
+            hs = hp.tile([P, CH], U8, name="hs", align_bytes=64)
+            nc.vector.quantize_mx(out=hw[:].bitcast(FP8X4), scales=hs[:], in_=live[("hg", c, n)][:])
+            live[("hw", c, n)] = hw
+            live[("hs", c, n)] = hs
+
+        def mm2(c, n, dg):
+            for kk in range(4):
+                acc = mp.tile([P, CH], F32, name="acc", tag="mp")
+                cols = slice((4 * dg + kk) * P, (4 * dg + kk + 1) * P)
+                nc.tensor.matmul_mx(out=acc[:], lhsT=w2w[:, n, cols].bitcast(FP8X4), lhsT_scale=w2s[:, n, cols],
+                                    rhs=live[("hw", c, n)][:].bitcast(FP8X4), rhs_scale=live[("hs", c, n)][:], start=True, stop=True)
+                live[("acc2", c, n, dg, kk)] = acc
+
+        def sig(c, n, dg):
+            for kk in range(4):
+                wT = wtp.tile([P, CH], F32, name="wT")
+                col = 8 * n + 4 * dg + kk
+                nc.scalar.activation(out=wT[:], in_=live[("acc2", c, n, dg, kk)][:], func=ACT.Sigmoid,
+                                     bias=bi[1][:, col:col + 1], scale=sc[1][:, col:col + 1])
+                live[("wT", c, n, dg, kk)] = wT
+
+        def t2(c, n, dg):
+            for bt in range(BT):
+                bank = tp.tile([P, CH], F32, name="tpb", tag="tp")
+                for kk in range(4):
+                    nc.tensor.transpose(bank[:, kk * P:(kk + 1) * P], live[("wT", c, n, dg, kk)][:, bt * P:(bt + 1) * P], ident[:])
+                live[("wps", c, n, dg, bt)] = bank
+
+        def prod(c, n, dg, bts):
+            key = ("o", c, dg) if n == 0 else ("p1", c, dg)
+            if key not in live:
+                live[key] = bigp.tile([P, BT, CH], F32, name="o", tag="big") if n == 0 else op.tile([P, BT, CH], F32, name="p1")
+            for bt in bts:
+                nc.vector.scalar_tensor_tensor(out=live[key][:, bt, :], in0=live[("wps", c, n, dg, bt)][:], scalar=3.0,
+                                               in1=t_sb[c][:, bt, n, dg * CH:(dg + 1) * CH], op0=ALU.mult, op1=ALU.mult)
+
+        def add(c, dg, bt, eng):
+            o = live[("o", c, dg)]
+            p1 = live[("p1", c, dg)]
+            if eng == "G":
+                nc.gpsimd.tensor_tensor(out=o[:, bt, :], in0=o[:, bt, :], in1=p1[:, bt, :], op=ALU.add)
+            else:
+                nc.vector.tensor_tensor(out=o[:, bt, :], in0=o[:, bt, :], in1=p1[:, bt, :], op=ALU.add)
+
+        def store(c, dg, bt0, nbt):
+            nc.sync.dma_start(out=out_v[:, c * BT + bt0:c * BT + bt0 + nbt, dg * CH:(dg + 1) * CH], in_=live[("o", c, dg)][:, bt0:bt0 + nbt, :])
+
+        ops = {"e1": e1, "s_add": s_add, "q1": q1, "w_evac": w_evac, "w_quant": w_quant, "prod": prod}
+
+        def run(items):
+            for it in items:
+                ops[it[0]](*it[1:])
+
+        def t1_run(c, sel, byhalf):
+            ks = [((g, sel) if byhalf else (sel, g)) for g in range(2)]
+            for n in (1, 0):
+                for (g, h) in ks:
+                    t1_bank(c, g, h, n)
+            return [("e1", c, g, h) for g, h in ks], [("s_add", c, g, h) for g, h in ks]
+
+        def w_run(kind, n, engs):
+            for a in range(2):
+                for b in range(2):
+                    w_bank(kind, n, a, b)
+            return [("w_evac", kind, n, a, b, engs[2 * a + b]) for a in range(2) for b in range(2)], [("w_quant", kind, n, 0), ("w_quant", kind, n, 1)]
+
+        def t2_run(c, n, dg):
+            t2(c, n, dg)
+            return [("prod", c, n, dg, (bt,)) for bt in range(BT)]
+
+        def adds(c, dg, pieces):
+            for bt in range(BT):
+                add(c, dg, bt, "G")
+                if pieces == 2 and bt % 2 == 1:
+                    store(c, dg, bt - 1, 2)
+            if pieces == 1:
+                store(c, dg, 0, BT)
+
+        make_identity(nc, ident[:])
+        nc.vector.memset(x1[:], 0.0)
+        nc.vector.memset(x2[:], 0.0)
+        load_params(0)
+        load_t(0, 2)
+        load_w1(0)
+        load_w1(1)
+        load_params(1)
+        load_w2(0)
+        params_cast(0)
+        s, v = t1_run(0, 0, True)
+        run(s)
+        run(v)
+        params_pe(0)
+        s, v = t1_run(0, 1, True)
+        run(s)
+        run(v)
+        q1(0, 0)
+        q1(0, 1)
+        ev, q = w_run(1, 0, "SVSV")
+        run(ev)
+        run(q)
+        load_w2(1)
+        load_t(1, 2)
+        load_t(2, 1)
+        load_t(3, 1)
+        ev, q = w_run(1, 1, "SVSV")
+        run(ev)
+        run(q)
+        params_cast(1)
+        for c in range(NCH + 1):
+            ok = c < NCH
+            nx = c + 1 < NCH
+            if c == 0:
+                mm1(c, 0)
+                relu(c, 0)
+                ev, q = w_run(2, 0, "VVVV")
+                run(ev)
+                run(q)
+                mm1(c, 1)
+                relu(c, 1)
+                ev, q = w_run(2, 1, "VSVS")
+                rg(c, 0)
+                run(ev[:2])
+                q2(c, 0)
+                run(ev[2:])
+                run(q)
+                params_pe(1)
+            else:
+                v = t2_run(c - 1, 1, 0)
+                if ok:
+                    mm1(c, 0)
+                    relu(c, 0)
+                run(v)
+                adds(c - 1, 0, 1 if ok else 2)
+                v = t2_run(c - 1, 1, 1)
+                if ok:
+                    mm1(c, 1)
+                    relu(c, 1)
+                    run(v[:2])
+                    rg(c, 0)
+                    run(v[2:])
+                    q2(c, 0)
+                    adds(c - 1, 1, 1)
+                else:
+                    for bt in range(BT):
+                        run(v[bt:bt + 1])
+                        add(c - 1, 1, bt, "V" if bt >= 2 else "G")
+                    store(c - 1, 1, 0, 2)
+                    store(c - 1, 1, 2, 2)
+            if not ok:
+                break
+            s, v = t1_run(c + 1, 0, c == 0) if nx else ([], [])
+            mm2(c, 0, 0)
+            run(s)
+            sig(c, 0, 0)
+            rg(c, 1)
+            run(v)
+            s, v = t1_run(c + 1, 1, c == 0) if nx else ([], [])
+            mm2(c, 0, 1)
+            run(s)
+            sig(c, 0, 1)
+            q2(c, 1)
+            run(v)
+            if nx:
+                q1(c + 1, 0)
+            v = t2_run(c, 0, 0)
+            mm2(c, 1, 0)
+            sig(c, 1, 0)
+            run(v[:2])
+            if nx:
+                q1(c + 1, 1)
+            run(v[2:])
+            v = t2_run(c, 0, 1)
+            mm2(c, 1, 1)
+            sig(c, 1, 1)
+            run(v)

@@ -17,6 +17,8 @@ EPS = 1e-5
 CH = 512
 NCH = B // CH
 BT = CH // P
+GP = 2
+LAG = 2
 FLOPS = 2 * B * DIM * NB * INTER * 2
 
 
@@ -25,14 +27,7 @@ def tile_af_2_pa_t_kernel(tc, t, W1, b1, g1, beta1, m1, v1, W2, b2, g2, beta2, m
     with ExitStack() as ctx:
         ctx.enter_context(tc.manual_schedule())
         const = ctx.enter_context(tc.tile_pool(name="const", bufs=1))
-        bigp = ctx.enter_context(tc.tile_pool(name="bigp", bufs=3))
-        wgrpp = ctx.enter_context(tc.tile_pool(name="wgrpp", bufs=4))
-        t1p = ctx.enter_context(tc.tile_pool(name="t1p", bufs=4))
-        sgp = ctx.enter_context(tc.tile_pool(name="sgp", bufs=2))
-        swp = ctx.enter_context(tc.tile_pool(name="swp", bufs=2))
-        hp = ctx.enter_context(tc.tile_pool(name="hp", bufs=2))
         wtp = ctx.enter_context(tc.tile_pool(name="wtp", bufs=12))
-        op = ctx.enter_context(tc.tile_pool(name="op", bufs=2))
         tp = ctx.enter_context(tc.psum_pool(name="tp", bufs=4))
         mp = ctx.enter_context(tc.psum_pool(name="mp", bufs=4))
 
@@ -44,6 +39,8 @@ def tile_af_2_pa_t_kernel(tc, t, W1, b1, g1, beta1, m1, v1, W2, b2, g2, beta2, m
         w1s = const.tile([P, 2, NB * INTER], U8, name="w1s", align_bytes=64)
         w2w = const.tile([P, NB, DIM], U32, name="w2w", align_bytes=64)
         w2s = const.tile([P, NB, DIM], U8, name="w2s", align_bytes=64)
+        hw = const.tile([P, NCH * NB, CH], U32, name="hw", align_bytes=64)
+        hs = const.tile([P, NCH * NB, CH], U8, name="hs", align_bytes=64)
         t_sb = [const.tile([P, BT, NB, DIM], BF16, name="t_sb%d" % c) for c in range(NCH)]
         x1 = const.tile([P, 256], BF16, name="x1")
         x2 = const.tile([P, P], BF16, name="x2")
@@ -61,24 +58,6 @@ def tile_af_2_pa_t_kernel(tc, t, W1, b1, g1, beta1, m1, v1, W2, b2, g2, beta2, m
             step = BT // pieces
             for i in range(pieces):
                 nc.sync.dma_start(out=t_sb[c][:, i * step:(i + 1) * step], in_=t_v[:, c * BT + i * step:c * BT + (i + 1) * step])
-
-        def load_w1(n):
-            raw = bigp.tile([P, 4096], BF16, name="wraw", tag="big")
-            nc.sync.dma_start(out=raw.rearrange("p (u x) -> p u x", u=2), in_=W1[n].rearrange("(u p e) d -> p u (e d)", u=2, p=P, e=2))
-            live[("w1raw", n)] = raw
-
-        def load_w2(n):
-            raw = bigp.tile([P, 4096], BF16, name="wraw", tag="big")
-            nc.sync.dma_start(out=raw.rearrange("p (k i) -> p k i", k=8), in_=W2[n].rearrange("(k p) i -> p k i", p=P))
-            live[("w2raw", n)] = raw
-
-        def load_params(stage):
-            if stage == 0:
-                for v, vec in enumerate((b1, g1, beta1, m1, v1)):
-                    nc.scalar.dma_start(out=x1[4 * v:4 * v + 4, :], in_=vec.rearrange("n (u c) -> (n u) c", c=256))
-            else:
-                for v, vec in enumerate((b2, g2, beta2, m2, v2)):
-                    nc.scalar.dma_start(out=x2[16 * v:16 * v + 16, :], in_=vec.rearrange("n (k c) -> (n k) c", c=P))
 
         def params_cast(stage):
             if stage == 0:
@@ -105,270 +84,262 @@ def tile_af_2_pa_t_kernel(tc, t, W1, b1, g1, beta1, m1, v1, W2, b2, g2, beta2, m
             nc.vector.tensor_tensor(out=df[stage][:], in0=df[stage][:], in1=sc[stage][:], op=ALU.mult)
             nc.vector.tensor_tensor(out=bi[stage][:], in0=df[stage][:], in1=q[:, 2, :], op=ALU.add)
 
-        def evac(eng, dst, src):
-            if eng == "S":
-                nc.scalar.copy(out=dst, in_=src)
-            else:
-                nc.vector.tensor_copy(out=dst, in_=src)
+        with ExitStack() as ph1:
+            rawp = ph1.enter_context(tc.tile_pool(name="rawp", bufs=3))
+            wgrpp = ph1.enter_context(tc.tile_pool(name="wgrpp", bufs=4))
+            t1p = ph1.enter_context(tc.tile_pool(name="t1p", bufs=4))
+            sgp = ph1.enter_context(tc.tile_pool(name="sgp", bufs=2))
+            swp = ph1.enter_context(tc.tile_pool(name="swp", bufs=2))
+            hp = ph1.enter_context(tc.tile_pool(name="hp", bufs=3))
 
-        def w_bank(kind, n, a, b):
-            bank = tp.tile([P, 2, 256], F32, name="tpb", tag="tp")
-            for x in range(2):
-                if kind == 1:
-                    words = live[("w1raw", n)][:, b * 2048 + x * 1024:b * 2048 + (x + 1) * 1024].bitcast(F32)[:, 256 * a:256 * a + 256]
+            def load_w1(n):
+                raw = rawp.tile([P, 4096], BF16, name="wraw")
+                nc.sync.dma_start(out=raw.rearrange("p (u x) -> p u x", u=2), in_=W1[n].rearrange("(u p e) d -> p u (e d)", u=2, p=P, e=2))
+                live[("w1raw", n)] = raw
+
+            def load_w2(n):
+                raw = rawp.tile([P, 4096], BF16, name="wraw")
+                nc.sync.dma_start(out=raw.rearrange("p (k i) -> p k i", k=8), in_=W2[n].rearrange("(k p) i -> p k i", p=P))
+                live[("w2raw", n)] = raw
+
+            def w_run(kind, n):
+                for a in range(2):
+                    for b in range(2):
+                        bank = tp.tile([P, 2, 256], F32, name="tpb", tag="tp")
+                        for x in range(2):
+                            if kind == 1:
+                                words = live[("w1raw", n)][:, b * 2048 + x * 1024:b * 2048 + (x + 1) * 1024].bitcast(F32)[:, 256 * a:256 * a + 256]
+                            else:
+                                k = 4 * a + 2 * b + x
+                                words = live[("w2raw", n)][:, k * 512:(k + 1) * 512].bitcast(F32)
+                            for u in range(2):
+                                nc.tensor.transpose(bank[:, u, x * P:(x + 1) * P], words[:, u * P:(u + 1) * P], ident[:])
+                        live[("wbank", a, b)] = bank
+
+            def w_evac(a, b, eng):
+                if b == 0:
+                    live[("wgrp", a)] = wgrpp.tile([P, 2048], BF16, name="wgrp", align_bytes=64)
+                dst = live[("wgrp", a)].bitcast(F32).rearrange("p (c u) -> p c u", u=2)[:, b * 256:(b + 1) * 256, :]
+                src = live[("wbank", a, b)].rearrange("p u c -> p c u")
+                if eng == "S":
+                    nc.scalar.copy(out=dst, in_=src)
                 else:
-                    k = 4 * a + 2 * b + x
-                    words = live[("w2raw", n)][:, k * 512:(k + 1) * 512].bitcast(F32)
-                for u in range(2):
-                    nc.tensor.transpose(bank[:, u, x * P:(x + 1) * P], words[:, u * P:(u + 1) * P], ident[:])
-            live[("wbank", kind, n, a, b)] = bank
+                    nc.vector.tensor_copy(out=dst, in_=src)
 
-        def w_evac(kind, n, a, b, eng):
-            if b == 0:
-                live[("wgrp", kind, n, a)] = wgrpp.tile([P, 2048], BF16, name="wgrp", align_bytes=64)
-            dst = live[("wgrp", kind, n, a)].bitcast(F32).rearrange("p (c u) -> p c u", u=2)[:, b * 256:(b + 1) * 256, :]
-            evac(eng, dst, live[("wbank", kind, n, a, b)].rearrange("p u c -> p c u"))
+            def w_quant(kind, n, a):
+                if kind == 1:
+                    cols = slice(n * 512, (n + 1) * 512)
+                    nc.vector.quantize_mx(out=w1w[:, a, cols].bitcast(FP8X4), scales=w1s[:, a, cols], in_=live[("wgrp", a)][:])
+                else:
+                    cols = slice(a * 512, (a + 1) * 512)
+                    nc.vector.quantize_mx(out=w2w[:, n, cols].bitcast(FP8X4), scales=w2s[:, n, cols], in_=live[("wgrp", a)][:])
 
-        def w_quant(kind, n, a):
-            grp = live[("wgrp", kind, n, a)]
-            if kind == 1:
-                cols = slice(n * 512, (n + 1) * 512)
-                nc.vector.quantize_mx(out=w1w[:, a, cols].bitcast(FP8X4), scales=w1s[:, a, cols], in_=grp[:])
-            else:
-                cols = slice(a * 512, (a + 1) * 512)
-                nc.vector.quantize_mx(out=w2w[:, n, cols].bitcast(FP8X4), scales=w2s[:, n, cols], in_=grp[:])
+            def t1_run(c, pairs):
+                for n in (1, 0):
+                    for (g, half) in pairs:
+                        bank = tp.tile([P, 2, 256], F32, name="tpb", tag="tp")
+                        for x in range(2):
+                            words = t_sb[c][:, 2 * half + x, n, :].bitcast(F32)
+                            for u in range(2):
+                                nc.tensor.transpose(bank[:, u, x * P:(x + 1) * P], words[:, 256 * g + u * P:256 * g + (u + 1) * P], ident[:])
+                        live[("tbank", g, half, n)] = bank
 
-        def t1_bank(c, g, half, n):
-            bank = tp.tile([P, 2, 256], F32, name="tpb", tag="tp")
-            for x in range(2):
-                words = t_sb[c][:, 2 * half + x, n, :].bitcast(F32)
-                for u in range(2):
-                    nc.tensor.transpose(bank[:, u, x * P:(x + 1) * P], words[:, 256 * g + u * P:256 * g + (u + 1) * P], ident[:])
-            live[("tbank", c, g, half, n)] = bank
+            def e1(g, half):
+                t1T = t1p.tile([P, 256, 2], F32, name="t1T")
+                nc.scalar.copy(out=t1T[:], in_=live[("tbank", g, half, 1)].rearrange("p u b -> p b u"))
+                live[("t1T", g, half)] = t1T
 
-        def e1(c, g, half):
-            t1T = t1p.tile([P, 256, 2], F32, name="t1T")
-            nc.scalar.copy(out=t1T[:], in_=live[("tbank", c, g, half, 1)].rearrange("p u b -> p b u"))
-            live[("t1T", c, g, half)] = t1T
+            def s_add(c, g, half):
+                if ("sg", c, g) not in live:
+                    live[("sg", c, g)] = sgp.tile([P, 2048], BF16, name="sg", align_bytes=64)
+                dst = live[("sg", c, g)][:, half * 1024:(half + 1) * 1024].rearrange("p (b u e) -> p b u e", u=2, e=2)
+                in0 = live[("tbank", g, half, 0)].rearrange("p u b -> p (u b)").bitcast(BF16).rearrange("p (u b e) -> p b u e", u=2, e=2)
+                in1 = live[("t1T", g, half)].rearrange("p b u -> p (b u)").bitcast(BF16).rearrange("p (b u e) -> p b u e", u=2, e=2)
+                nc.vector.tensor_tensor(out=dst, in0=in0, in1=in1, op=ALU.add)
 
-        def s_add(c, g, half):
-            if ("sg", c, g) not in live:
-                live[("sg", c, g)] = sgp.tile([P, 2048], BF16, name="sg", align_bytes=64)
-            dst = live[("sg", c, g)][:, half * 1024:(half + 1) * 1024].rearrange("p (b u e) -> p b u e", u=2, e=2)
-            in0 = live[("tbank", c, g, half, 0)].rearrange("p u b -> p (u b)").bitcast(BF16).rearrange("p (u b e) -> p b u e", u=2, e=2)
-            in1 = live[("t1T", c, g, half)].rearrange("p b u -> p (b u)").bitcast(BF16).rearrange("p (b u e) -> p b u e", u=2, e=2)
-            nc.vector.tensor_tensor(out=dst, in0=in0, in1=in1, op=ALU.add)
+            def q1(c, g):
+                if ("sw", c) not in live:
+                    live[("sw", c)] = swp.tile([P, 2, CH], U32, name="sw", align_bytes=64)
+                    live[("ss", c)] = swp.tile([P, 2, CH], U8, name="ss", align_bytes=64)
+                nc.vector.quantize_mx(out=live[("sw", c)][:, g, :].bitcast(FP8X4), scales=live[("ss", c)][:, g, :], in_=live[("sg", c, g)][:])
 
-        def q1(c, g):
-            if ("sw", c) not in live:
-                live[("sw", c)] = swp.tile([P, 2, CH], U32, name="sw", align_bytes=64)
-                live[("ss", c)] = swp.tile([P, 2, CH], U8, name="ss", align_bytes=64)
-            nc.vector.quantize_mx(out=live[("sw", c)][:, g, :].bitcast(FP8X4), scales=live[("ss", c)][:, g, :], in_=live[("sg", c, g)][:])
+            def mm1(j):
+                c, n = j // 2, j % 2
+                for tt in range(4):
+                    acc = mp.tile([P, CH], F32, name="acc", tag="mp")
+                    cols = slice(n * 512 + tt * P, n * 512 + (tt + 1) * P)
+                    for g in range(2):
+                        nc.tensor.matmul_mx(out=acc[:], lhsT=w1w[:, g, cols].bitcast(FP8X4), lhsT_scale=w1s[:, g, cols],
+                                            rhs=live[("sw", c)][:, g, :].bitcast(FP8X4), rhs_scale=live[("ss", c)][:, g, :],
+                                            start=(g == 0), stop=(g == 1))
+                    live[("acc1", tt)] = acc
 
-        def mm1(c, n):
-            for tt in range(4):
-                acc = mp.tile([P, CH], F32, name="acc", tag="mp")
-                cols = slice(n * 512 + tt * P, n * 512 + (tt + 1) * P)
+            def relu(j):
+                n = j % 2
+                hT = hp.tile([P, 4, CH], BF16, name="hT")
+                for tt in range(4):
+                    col = (tt % 2) * 4 + 2 * n + tt // 2
+                    nc.scalar.activation(out=hT[:, tt, :], in_=live[("acc1", tt)][:], func=ACT.Relu,
+                                         bias=bi[0][:, col:col + 1], scale=sc[0][:, col:col + 1])
+                live[("hT", j)] = hT
+
+            def rg(j):
+                hg = hp.tile([P, 4 * CH], BF16, name="hg", align_bytes=64)
+                nc.vector.tensor_copy(out=hg.rearrange("p (c i t) -> p c t i", i=4, t=4), in_=live[("hT", j)].rearrange("p t (c i) -> p c t i", i=4))
+                live[("hg", j)] = hg
+
+            def q2(j):
+                nc.vector.quantize_mx(out=hw[:, j, :].bitcast(FP8X4), scales=hs[:, j, :], in_=live[("hg", j)][:])
+
+            make_identity(nc, ident[:])
+            nc.vector.memset(x1[:], 0.0)
+            nc.vector.memset(x2[:], 0.0)
+            for v, vec in enumerate((b1, g1, beta1, m1, v1)):
+                nc.scalar.dma_start(out=x1[4 * v:4 * v + 4, :], in_=vec.rearrange("n (u c) -> (n u) c", c=256))
+            load_t(0, 2)
+            load_w1(0)
+            load_w1(1)
+            load_t(1, 2)
+            load_t(2, 1)
+            load_t(3, 1)
+            load_w2(0)
+            params_cast(0)
+            for half in range(2):
+                t1_run(0, [(0, half), (1, half)])
                 for g in range(2):
-                    nc.tensor.matmul_mx(out=acc[:], lhsT=w1w[:, g, cols].bitcast(FP8X4), lhsT_scale=w1s[:, g, cols],
-                                        rhs=live[("sw", c)][:, g, :].bitcast(FP8X4), rhs_scale=live[("ss", c)][:, g, :],
-                                        start=(g == 0), stop=(g == 1))
-                live[("acc1", c, n, tt)] = acc
+                    e1(g, half)
+                for g in range(2):
+                    s_add(0, g, half)
+                if half == 0:
+                    params_pe(0)
+            q1(0, 0)
+            q1(0, 1)
+            for n in range(2):
+                w_run(1, n)
+                for a in range(2):
+                    for b in range(2):
+                        w_evac(a, b, "V" if (a, b) == (1, 1) else "S")
+                w_quant(1, n, 0)
+                w_quant(1, n, 1)
+                if n == 0:
+                    load_w2(1)
+                    for v, vec in enumerate((b2, g2, beta2, m2, v2)):
+                        nc.sync.dma_start(out=x2[16 * v:16 * v + 16, :], in_=vec.rearrange("n (k c) -> (n k) c", c=P))
+            for j in range(2 * NCH):
+                c, n = j // 2, j % 2
+                if j < 2:
+                    mm1(j)
+                    t1_run(1, [(0, j), (1, j)])
+                    relu(j)
+                    for g in range(2):
+                        e1(g, j)
+                    if j == 1:
+                        rg(0)
+                    for g in range(2):
+                        s_add(1, g, j)
+                    if j == 1:
+                        q1(1, 0)
+                        q1(1, 1)
+                        q2(0)
+                elif j < 6:
+                    t1_run(c + 1, [(n, 0), (n, 1)])
+                    mm1(j)
+                    for half in range(2):
+                        e1(n, half)
+                    relu(j)
+                    rg(j - 1)
+                    for half in range(2):
+                        s_add(c + 1, n, half)
+                    if n == 1:
+                        q1(c + 1, 0)
+                    q2(j - 1)
+                    if n == 1:
+                        q1(c + 1, 1)
+                else:
+                    w_run(2, j - 6)
+                    mm1(j)
+                    w_evac(0, 0, "S")
+                    w_evac(1, 0, "S")
+                    relu(j)
+                    rg(j - 1)
+                    w_evac(0, 1, "V")
+                    w_evac(1, 1, "V")
+                    q2(j - 1)
+                    w_quant(2, j - 6, 0)
+                    w_quant(2, j - 6, 1)
+                    if j == 6:
+                        params_cast(1)
+                        params_pe(1)
+            rg(2 * NCH - 1)
+            q2(2 * NCH - 1)
 
-        def relu(c, n):
-            hT = hp.tile([P, 4, CH], BF16, name="hT")
-            for tt in range(4):
-                col = (tt % 2) * 4 + 2 * n + tt // 2
-                nc.scalar.activation(out=hT[:, tt, :], in_=live[("acc1", c, n, tt)][:], func=ACT.Relu,
-                                     bias=bi[0][:, col:col + 1], scale=sc[0][:, col:col + 1])
-            live[("hT", c, n)] = hT
+        with ExitStack() as ph2:
+            op = ph2.enter_context(tc.tile_pool(name="op", bufs=3))
+            pp = ph2.enter_context(tc.tile_pool(name="pp", bufs=2))
 
-        def rg(c, n, eng="V"):
-            hg = hp.tile([P, 4 * CH], BF16, name="hg", align_bytes=64)
-            dst = hg.rearrange("p (c i t) -> p c t i", i=4, t=4)
-            src = live[("hT", c, n)].rearrange("p t (c i) -> p c t i", i=4)
-            if eng == "V":
-                nc.vector.tensor_copy(out=dst, in_=src)
-            elif eng == "G":
-                nc.gpsimd.tensor_scalar(out=dst, in0=src, scalar1=1.0, scalar2=0.0, op0=ALU.mult, op1=ALU.add)
-            else:
-                nc.scalar.copy(out=dst, in_=src)
-            live[("hg", c, n)] = hg
-
-        def q2(c, n):
-            hw = hp.tile([P, CH], U32, name="hw", align_bytes=64)
-            hs = hp.tile([P, CH], U8, name="hs", align_bytes=64)
-            nc.vector.quantize_mx(out=hw[:].bitcast(FP8X4), scales=hs[:], in_=live[("hg", c, n)][:])
-            live[("hw", c, n)] = hw
-            live[("hs", c, n)] = hs
-
-        def mm2(c, n, dg):
-            for kk in range(4):
-                acc = mp.tile([P, CH], F32, name="acc", tag="mp")
-                cols = slice((4 * dg + kk) * P, (4 * dg + kk + 1) * P)
-                nc.tensor.matmul_mx(out=acc[:], lhsT=w2w[:, n, cols].bitcast(FP8X4), lhsT_scale=w2s[:, n, cols],
-                                    rhs=live[("hw", c, n)][:].bitcast(FP8X4), rhs_scale=live[("hs", c, n)][:], start=True, stop=True)
-                live[("acc2", c, n, dg, kk)] = acc
-
-        def sig(c, n, dg):
-            for kk in range(4):
-                wT = wtp.tile([P, CH], F32, name="wT")
-                col = 8 * n + 4 * dg + kk
-                nc.scalar.activation(out=wT[:], in_=live[("acc2", c, n, dg, kk)][:], func=ACT.Sigmoid,
-                                     bias=bi[1][:, col:col + 1], scale=sc[1][:, col:col + 1])
-                live[("wT", c, n, dg, kk)] = wT
-
-        def t2(c, n, dg):
-            for bt in range(BT):
-                bank = tp.tile([P, CH], F32, name="tpb", tag="tp")
+            def mm2(c, n, dg):
                 for kk in range(4):
-                    nc.tensor.transpose(bank[:, kk * P:(kk + 1) * P], live[("wT", c, n, dg, kk)][:, bt * P:(bt + 1) * P], ident[:])
-                live[("wps", c, n, dg, bt)] = bank
+                    acc = mp.tile([P, CH], F32, name="acc", tag="mp")
+                    cols = slice((4 * dg + kk) * P, (4 * dg + kk + 1) * P)
+                    nc.tensor.matmul_mx(out=acc[:], lhsT=w2w[:, n, cols].bitcast(FP8X4), lhsT_scale=w2s[:, n, cols],
+                                        rhs=hw[:, 2 * c + n, :].bitcast(FP8X4), rhs_scale=hs[:, 2 * c + n, :], start=True, stop=True)
+                    live[("acc2", kk)] = acc
 
-        def prod(c, n, dg, bts):
-            key = ("o", c, dg) if n == 0 else ("p1", c, dg)
-            if key not in live:
-                live[key] = bigp.tile([P, BT, CH], F32, name="o", tag="big") if n == 0 else op.tile([P, BT, CH], F32, name="p1")
-            for bt in bts:
-                nc.vector.scalar_tensor_tensor(out=live[key][:, bt, :], in0=live[("wps", c, n, dg, bt)][:], scalar=3.0,
+            def sig(c, n, dg):
+                for kk in range(4):
+                    wT = wtp.tile([P, CH], F32, name="wT")
+                    col = 8 * n + 4 * dg + kk
+                    nc.scalar.activation(out=wT[:], in_=live[("acc2", kk)][:], func=ACT.Sigmoid,
+                                         bias=bi[1][:, col:col + 1], scale=sc[1][:, col:col + 1])
+                    live[("wT", c, n, dg, kk)] = wT
+
+            def t2(c, n, dg):
+                for bt in range(BT):
+                    bank = tp.tile([P, CH], F32, name="tpb", tag="tp")
+                    for kk in range(4):
+                        nc.tensor.transpose(bank[:, kk * P:(kk + 1) * P], live[("wT", c, n, dg, kk)][:, bt * P:(bt + 1) * P], ident[:])
+                    live[("wps", bt)] = bank
+
+            def prod(c, n, dg, bt):
+                if bt == 0:
+                    if n == 0:
+                        live["o"] = op.tile([P, BT, CH], F32, name="o")
+                    else:
+                        live["p1"] = pp.tile([P, BT, CH], F32, name="p1")
+                dst = live["o"] if n == 0 else live["p1"]
+                nc.vector.scalar_tensor_tensor(out=dst[:, bt, :], in0=live[("wps", bt)][:], scalar=3.0,
                                                in1=t_sb[c][:, bt, n, dg * CH:(dg + 1) * CH], op0=ALU.mult, op1=ALU.mult)
 
-        def add(c, dg, bt, eng):
-            o = live[("o", c, dg)]
-            p1 = live[("p1", c, dg)]
-            if eng == "G":
-                nc.gpsimd.tensor_tensor(out=o[:, bt, :], in0=o[:, bt, :], in1=p1[:, bt, :], op=ALU.add)
-            else:
-                nc.vector.tensor_tensor(out=o[:, bt, :], in0=o[:, bt, :], in1=p1[:, bt, :], op=ALU.add)
-
-        def store(c, dg, bt0, nbt):
-            nc.sync.dma_start(out=out_v[:, c * BT + bt0:c * BT + bt0 + nbt, dg * CH:(dg + 1) * CH], in_=live[("o", c, dg)][:, bt0:bt0 + nbt, :])
-
-        ops = {"e1": e1, "s_add": s_add, "q1": q1, "w_evac": w_evac, "w_quant": w_quant, "prod": prod}
-
-        def run(items):
-            for it in items:
-                ops[it[0]](*it[1:])
-
-        def t1_run(c, sel, byhalf):
-            ks = [((g, sel) if byhalf else (sel, g)) for g in range(2)]
-            for n in (1, 0):
-                for (g, h) in ks:
-                    t1_bank(c, g, h, n)
-            return [("e1", c, g, h) for g, h in ks], [("s_add", c, g, h) for g, h in ks]
-
-        def w_run(kind, n, engs):
-            for a in range(2):
-                for b in range(2):
-                    w_bank(kind, n, a, b)
-            return [("w_evac", kind, n, a, b, engs[2 * a + b]) for a in range(2) for b in range(2)], [("w_quant", kind, n, 0), ("w_quant", kind, n, 1)]
-
-        def t2_run(c, n, dg):
-            t2(c, n, dg)
-            return [("prod", c, n, dg, (bt,)) for bt in range(BT)]
-
-        def adds(c, dg, pieces):
-            for bt in range(BT):
-                add(c, dg, bt, "G")
-                if pieces == 2 and bt % 2 == 1:
-                    store(c, dg, bt - 1, 2)
-            if pieces == 1:
-                store(c, dg, 0, BT)
-
-        make_identity(nc, ident[:])
-        nc.vector.memset(x1[:], 0.0)
-        nc.vector.memset(x2[:], 0.0)
-        load_params(0)
-        load_t(0, 2)
-        load_w1(0)
-        load_w1(1)
-        load_params(1)
-        load_w2(0)
-        params_cast(0)
-        s, v = t1_run(0, 0, True)
-        run(s)
-        run(v)
-        params_pe(0)
-        s, v = t1_run(0, 1, True)
-        run(s)
-        run(v)
-        q1(0, 0)
-        q1(0, 1)
-        ev, q = w_run(1, 0, "SVSV")
-        run(ev)
-        run(q)
-        load_w2(1)
-        load_t(1, 2)
-        load_t(2, 1)
-        load_t(3, 1)
-        ev, q = w_run(1, 1, "SVSV")
-        run(ev)
-        run(q)
-        params_cast(1)
-        for c in range(NCH + 1):
-            ok = c < NCH
-            nx = c + 1 < NCH
-            if c == 0:
-                mm1(c, 0)
-                relu(c, 0)
-                ev, q = w_run(2, 0, "VVVV")
-                run(ev)
-                run(q)
-                mm1(c, 1)
-                relu(c, 1)
-                ev, q = w_run(2, 1, "VSVS")
-                rg(c, 0)
-                run(ev[:2])
-                q2(c, 0)
-                run(ev[2:])
-                run(q)
-                params_pe(1)
-            else:
-                v = t2_run(c - 1, 1, 0)
-                if ok:
-                    mm1(c, 0)
-                    relu(c, 0)
-                run(v)
-                adds(c - 1, 0, 1 if ok else 2)
-                v = t2_run(c - 1, 1, 1)
-                if ok:
-                    mm1(c, 1)
-                    relu(c, 1)
-                    run(v[:2])
-                    rg(c, 0)
-                    run(v[2:])
-                    q2(c, 0)
-                    adds(c - 1, 1, 1)
+            def add(bt, eng):
+                o = live["o"]
+                p1 = live["p1"]
+                if eng == "G":
+                    for x in range(GP):
+                        cols = slice(x * (CH // GP), (x + 1) * (CH // GP))
+                        nc.gpsimd.tensor_tensor(out=o[:, bt, cols], in0=o[:, bt, cols], in1=p1[:, bt, cols], op=ALU.add)
                 else:
+                    nc.vector.tensor_tensor(out=o[:, bt, :], in0=o[:, bt, :], in1=p1[:, bt, :], op=ALU.add)
+
+            def store(c, dg, bt0, nbt):
+                nc.sync.dma_start(out=out_v[:, c * BT + bt0:c * BT + bt0 + nbt, dg * CH:(dg + 1) * CH], in_=live["o"][:, bt0:bt0 + nbt, :])
+
+            units = [(c, n, dg) for c in range(NCH) for dg in range(2) for n in range(NB)]
+            for k in range(len(units) + LAG):
+                if k >= LAG:
+                    t2(*units[k - LAG])
+                if k < len(units):
+                    mm2(*units[k])
+                    sig(*units[k])
+                if k >= LAG:
+                    c, n, dg = units[k - LAG]
+                    last = k == len(units) + LAG - 1
                     for bt in range(BT):
-                        run(v[bt:bt + 1])
-                        add(c - 1, 1, bt, "V" if bt >= 2 else "G")
-                    store(c - 1, 1, 0, 2)
-                    store(c - 1, 1, 2, 2)
-            if not ok:
-                break
-            s, v = t1_run(c + 1, 0, c == 0) if nx else ([], [])
-            mm2(c, 0, 0)
-            run(s)
-            sig(c, 0, 0)
-            rg(c, 1)
-            run(v)
-            s, v = t1_run(c + 1, 1, c == 0) if nx else ([], [])
-            mm2(c, 0, 1)
-            run(s)
-            sig(c, 0, 1)
-            q2(c, 1)
-            run(v)
-            if nx:
-                q1(c + 1, 0)
-            v = t2_run(c, 0, 0)
-            mm2(c, 1, 0)
-            sig(c, 1, 0)
-            run(v[:2])
-            if nx:
-                q1(c + 1, 1)
-            run(v[2:])
-            v = t2_run(c, 0, 1)
-            mm2(c, 1, 1)
-            sig(c, 1, 1)
-            run(v)
+                        prod(c, n, dg, bt)
+                        if last:
+                            add(bt, "V")
+                            if bt % 2 == 1:
+                                store(c, dg, bt - 1, 2)
+                    if n == 1 and not last:
+                        for bt in range(BT):
+                            add(bt, "G")
+                        store(c, dg, 0, BT)

@@ -17,7 +17,7 @@ EPS = 1e-5
 CH = 512
 NCH = B // CH
 BT = CH // P
-GP = 2
+GP = 1
 LAG = 2
 FLOPS = 2 * B * DIM * NB * INTER * 2
 
@@ -83,6 +83,24 @@ def tile_af_2_pa_t_kernel(tc, t, W1, b1, g1, beta1, m1, v1, W2, b2, g2, beta2, m
             nc.vector.tensor_tensor(out=df[stage][:], in0=q[:, 0, :], in1=q[:, 3, :], op=ALU.subtract)
             nc.vector.tensor_tensor(out=df[stage][:], in0=df[stage][:], in1=sc[stage][:], op=ALU.mult)
             nc.vector.tensor_tensor(out=bi[stage][:], in0=df[stage][:], in1=q[:, 2, :], op=ALU.add)
+
+        def mm2(c, n, dg):
+            for kk in range(4):
+                acc = mp.tile([P, CH], F32, name="acc", tag="mp")
+                cols = slice((4 * dg + kk) * P, (4 * dg + kk + 1) * P)
+                nc.tensor.matmul_mx(out=acc[:], lhsT=w2w[:, n, cols].bitcast(FP8X4), lhsT_scale=w2s[:, n, cols],
+                                    rhs=hw[:, 2 * c + n, :].bitcast(FP8X4), rhs_scale=hs[:, 2 * c + n, :], start=True, stop=True)
+                live[("acc2", kk)] = acc
+
+        def sig(c, n, dg):
+            for kk in range(4):
+                wT = wtp.tile([P, CH], F32, name="wT")
+                col = 8 * n + 4 * dg + kk
+                nc.scalar.activation(out=wT[:], in_=live[("acc2", kk)][:], func=ACT.Sigmoid,
+                                     bias=bi[1][:, col:col + 1], scale=sc[1][:, col:col + 1])
+                live[("wT", c, n, dg, kk)] = wT
+
+        units = [(c, n, dg) for c in range(NCH) for dg in range(2) for n in range(NB)]
 
         with ExitStack() as ph1:
             rawp = ph1.enter_context(tc.tile_pool(name="rawp", bufs=3))
@@ -261,37 +279,27 @@ def tile_af_2_pa_t_kernel(tc, t, W1, b1, g1, beta1, m1, v1, W2, b2, g2, beta2, m
                     w_evac(0, 0, "S")
                     w_evac(1, 0, "S")
                     relu(j)
-                    rg(j - 1)
                     w_evac(0, 1, "V")
                     w_evac(1, 1, "V")
-                    q2(j - 1)
+                    if j == 6:
+                        params_cast(1)
                     w_quant(2, j - 6, 0)
                     w_quant(2, j - 6, 1)
                     if j == 6:
-                        params_cast(1)
                         params_pe(1)
-            rg(2 * NCH - 1)
-            q2(2 * NCH - 1)
+            for k in range(LAG):
+                mm2(*units[k])
+                sig(*units[k])
+            rg(5)
+            rg(6)
+            q2(5)
+            rg(7)
+            q2(6)
+            q2(7)
 
         with ExitStack() as ph2:
             op = ph2.enter_context(tc.tile_pool(name="op", bufs=3))
             pp = ph2.enter_context(tc.tile_pool(name="pp", bufs=2))
-
-            def mm2(c, n, dg):
-                for kk in range(4):
-                    acc = mp.tile([P, CH], F32, name="acc", tag="mp")
-                    cols = slice((4 * dg + kk) * P, (4 * dg + kk + 1) * P)
-                    nc.tensor.matmul_mx(out=acc[:], lhsT=w2w[:, n, cols].bitcast(FP8X4), lhsT_scale=w2s[:, n, cols],
-                                        rhs=hw[:, 2 * c + n, :].bitcast(FP8X4), rhs_scale=hs[:, 2 * c + n, :], start=True, stop=True)
-                    live[("acc2", kk)] = acc
-
-            def sig(c, n, dg):
-                for kk in range(4):
-                    wT = wtp.tile([P, CH], F32, name="wT")
-                    col = 8 * n + 4 * dg + kk
-                    nc.scalar.activation(out=wT[:], in_=live[("acc2", kk)][:], func=ACT.Sigmoid,
-                                         bias=bi[1][:, col:col + 1], scale=sc[1][:, col:col + 1])
-                    live[("wT", c, n, dg, kk)] = wT
 
             def t2(c, n, dg):
                 for bt in range(BT):
@@ -323,8 +331,7 @@ def tile_af_2_pa_t_kernel(tc, t, W1, b1, g1, beta1, m1, v1, W2, b2, g2, beta2, m
             def store(c, dg, bt0, nbt):
                 nc.sync.dma_start(out=out_v[:, c * BT + bt0:c * BT + bt0 + nbt, dg * CH:(dg + 1) * CH], in_=live["o"][:, bt0:bt0 + nbt, :])
 
-            units = [(c, n, dg) for c in range(NCH) for dg in range(2) for n in range(NB)]
-            for k in range(len(units) + LAG):
+            for k in range(LAG, len(units) + LAG):
                 if k >= LAG:
                     t2(*units[k - LAG])
                 if k < len(units):
@@ -335,10 +342,13 @@ def tile_af_2_pa_t_kernel(tc, t, W1, b1, g1, beta1, m1, v1, W2, b2, g2, beta2, m
                     last = k == len(units) + LAG - 1
                     for bt in range(BT):
                         prod(c, n, dg, bt)
-                        if last:
-                            add(bt, "V")
-                            if bt % 2 == 1:
-                                store(c, dg, bt - 1, 2)
+                        if last and bt < 2:
+                            add(bt, "G")
+                    if last:
+                        store(c, dg, 0, 2)
+                        add(2, "V")
+                        add(3, "V")
+                        store(c, dg, 2, 2)
                     if n == 1 and not last:
                         for bt in range(BT):
                             add(bt, "G")

@@ -105,7 +105,7 @@ def tile_af_2_pa_t_kernel(tc, t, W1, b1, g1, beta1, m1, v1, W2, b2, g2, beta2, m
         with ExitStack() as ph1:
             rawp = ph1.enter_context(tc.tile_pool(name="rawp", bufs=3))
             wgrpp = ph1.enter_context(tc.tile_pool(name="wgrpp", bufs=4))
-            t1p = ph1.enter_context(tc.tile_pool(name="t1p", bufs=4))
+            ssp = ph1.enter_context(tc.tile_pool(name="ssp", bufs=2))
             sgp = ph1.enter_context(tc.tile_pool(name="sgp", bufs=2))
             swp = ph1.enter_context(tc.tile_pool(name="swp", bufs=2))
             hp = ph1.enter_context(tc.tile_pool(name="hp", bufs=3))
@@ -152,28 +152,26 @@ def tile_af_2_pa_t_kernel(tc, t, W1, b1, g1, beta1, m1, v1, W2, b2, g2, beta2, m
                     cols = slice(a * 512, (a + 1) * 512)
                     nc.vector.quantize_mx(out=w2w[:, n, cols].bitcast(FP8X4), scales=w2s[:, n, cols], in_=live[("wgrp", a)][:])
 
+            def s_add(c, half):
+                if half == 0:
+                    live[("s", c)] = ssp.tile([P, BT, DIM], BF16, name="s_sb")
+                rows = slice(2 * half, 2 * half + 2)
+                nc.vector.tensor_tensor(out=live[("s", c)][:, rows, :], in0=t_sb[c][:, rows, 0, :], in1=t_sb[c][:, rows, 1, :], op=ALU.add)
+
             def t1_run(c, pairs):
-                for n in (1, 0):
-                    for (g, half) in pairs:
-                        bank = tp.tile([P, 2, 256], F32, name="tpb", tag="tp")
-                        for x in range(2):
-                            words = t_sb[c][:, 2 * half + x, n, :].bitcast(F32)
-                            for u in range(2):
-                                nc.tensor.transpose(bank[:, u, x * P:(x + 1) * P], words[:, 256 * g + u * P:256 * g + (u + 1) * P], ident[:])
-                        live[("tbank", g, half, n)] = bank
+                for (g, half) in pairs:
+                    bank = tp.tile([P, 2, 256], F32, name="tpb", tag="tp")
+                    for x in range(2):
+                        words = live[("s", c)][:, 2 * half + x, :].bitcast(F32)
+                        for u in range(2):
+                            nc.tensor.transpose(bank[:, u, x * P:(x + 1) * P], words[:, 256 * g + u * P:256 * g + (u + 1) * P], ident[:])
+                    live[("tbank", g, half)] = bank
 
-            def e1(g, half):
-                t1T = t1p.tile([P, 256, 2], F32, name="t1T")
-                nc.scalar.copy(out=t1T[:], in_=live[("tbank", g, half, 1)].rearrange("p u b -> p b u"))
-                live[("t1T", g, half)] = t1T
-
-            def s_add(c, g, half):
+            def e1(c, g, half):
                 if ("sg", c, g) not in live:
                     live[("sg", c, g)] = sgp.tile([P, 2048], BF16, name="sg", align_bytes=64)
-                dst = live[("sg", c, g)][:, half * 1024:(half + 1) * 1024].rearrange("p (b u e) -> p b u e", u=2, e=2)
-                in0 = live[("tbank", g, half, 0)].rearrange("p u b -> p (u b)").bitcast(BF16).rearrange("p (u b e) -> p b u e", u=2, e=2)
-                in1 = live[("t1T", g, half)].rearrange("p b u -> p (b u)").bitcast(BF16).rearrange("p (b u e) -> p b u e", u=2, e=2)
-                nc.vector.tensor_tensor(out=dst, in0=in0, in1=in1, op=ALU.add)
+                dst = live[("sg", c, g)].bitcast(F32).rearrange("p (b u) -> p b u", u=2)[:, half * 256:(half + 1) * 256, :]
+                nc.scalar.copy(out=dst, in_=live[("tbank", g, half)].rearrange("p u b -> p b u"))
 
             def q1(c, g):
                 if ("sw", c) not in live:
@@ -223,11 +221,10 @@ def tile_af_2_pa_t_kernel(tc, t, W1, b1, g1, beta1, m1, v1, W2, b2, g2, beta2, m
             load_w2(0)
             params_cast(0)
             for half in range(2):
+                s_add(0, half)
                 t1_run(0, [(0, half), (1, half)])
                 for g in range(2):
-                    e1(g, half)
-                for g in range(2):
-                    s_add(0, g, half)
+                    e1(0, g, half)
                 if half == 0:
                     params_pe(0)
             q1(0, 0)
@@ -247,32 +244,33 @@ def tile_af_2_pa_t_kernel(tc, t, W1, b1, g1, beta1, m1, v1, W2, b2, g2, beta2, m
                 c, n = j // 2, j % 2
                 if j < 2:
                     mm1(j)
+                    s_add(1, j)
                     t1_run(1, [(0, j), (1, j)])
                     relu(j)
                     for g in range(2):
-                        e1(g, j)
+                        e1(1, g, j)
                     if j == 1:
                         rg(0)
-                    for g in range(2):
-                        s_add(1, g, j)
-                    if j == 1:
                         q1(1, 0)
                         q1(1, 1)
                         q2(0)
+                        for half in range(2):
+                            s_add(2, half)
                 elif j < 6:
                     t1_run(c + 1, [(n, 0), (n, 1)])
                     mm1(j)
                     for half in range(2):
-                        e1(n, half)
+                        e1(c + 1, n, half)
                     relu(j)
                     rg(j - 1)
-                    for half in range(2):
-                        s_add(c + 1, n, half)
                     if n == 1:
                         q1(c + 1, 0)
                     q2(j - 1)
                     if n == 1:
                         q1(c + 1, 1)
+                        if j == 3:
+                            for half in range(2):
+                                s_add(3, half)
                 else:
                     w_run(2, j - 6)
                     mm1(j)

@@ -17,7 +17,6 @@ EPS = 1e-5
 CH = 512
 NCH = B // CH
 BT = CH // P
-GP = 1
 LAG = 2
 FLOPS = 2 * B * DIM * NB * INTER * 2
 
@@ -46,6 +45,8 @@ def tile_af_2_pa_t_kernel(tc, t, W1, b1, g1, beta1, m1, v1, W2, b2, g2, beta2, m
         x2 = const.tile([P, P], BF16, name="x2")
         xf1 = const.tile([P, 2, P], F32, name="xf1")
         xf2 = const.tile([P, P], F32, name="xf2")
+        mhalf = const.tile([P, 16], F32, name="mhalf")
+        dummy = const.tile([P, 1], F32, name="dummy")
         pr = [const.tile([P, 5, 8], F32, name="pr1"), const.tile([P, 5, 16], F32, name="pr2")]
         sc = [const.tile([P, 8], F32, name="sc1"), const.tile([P, 16], F32, name="sc2")]
         bi = [const.tile([P, 8], F32, name="bi1"), const.tile([P, 16], F32, name="bi2")]
@@ -54,16 +55,22 @@ def tile_af_2_pa_t_kernel(tc, t, W1, b1, g1, beta1, m1, v1, W2, b2, g2, beta2, m
 
         live = {}
 
-        def load_t(c, pieces):
-            step = BT // pieces
-            for i in range(pieces):
-                nc.sync.dma_start(out=t_sb[c][:, i * step:(i + 1) * step], in_=t_v[:, c * BT + i * step:c * BT + (i + 1) * step])
+        def load_t(c, bt0, nbt):
+            nc.sync.dma_start(out=t_sb[c][:, bt0:bt0 + nbt], in_=t_v[:, c * BT + bt0:c * BT + bt0 + nbt])
+
+        def load_params(stage):
+            vecs = ((b1, g1, beta1, m1, v1), (b2, g2, beta2, m2, v2))[stage]
+            for v, vec in enumerate(vecs):
+                if stage == 0:
+                    nc.sync.dma_start(out=x1[4 * v:4 * v + 4, :], in_=vec.rearrange("n (u c) -> (n u) c", c=256))
+                else:
+                    nc.sync.dma_start(out=x2[16 * v:16 * v + 16, :], in_=vec.rearrange("n (k c) -> (n k) c", c=P))
 
         def params_cast(stage):
             if stage == 0:
-                nc.vector.tensor_copy(out=xf1[:], in_=x1.rearrange("r (p e) -> r e p", e=2))
+                nc.gpsimd.tensor_copy(out=xf1[:], in_=x1.rearrange("r (p e) -> r e p", e=2))
             else:
-                nc.vector.tensor_copy(out=xf2[:], in_=x2[:])
+                nc.gpsimd.tensor_copy(out=xf2[:], in_=x2[:])
 
         def params_pe(stage):
             if stage == 0:
@@ -76,13 +83,12 @@ def tile_af_2_pa_t_kernel(tc, t, W1, b1, g1, beta1, m1, v1, W2, b2, g2, beta2, m
                 nc.tensor.transpose(bank[:], xf2[:], ident[:])
                 nc.vector.tensor_copy(out=pr[1][:], in_=bank[:, 0:80].rearrange("p (v j) -> p v j", v=5))
             q = pr[stage]
-            nc.vector.tensor_scalar_add(out=rs[stage][:], in0=q[:, 4, :], scalar1=EPS)
-            nc.scalar.sqrt(out=rs[stage][:], in_=rs[stage][:])
-            nc.vector.reciprocal(out=rs[stage][:], in_=rs[stage][:])
-            nc.vector.tensor_tensor(out=sc[stage][:], in0=q[:, 1, :], in1=rs[stage][:], op=ALU.mult)
-            nc.vector.tensor_tensor(out=df[stage][:], in0=q[:, 0, :], in1=q[:, 3, :], op=ALU.subtract)
-            nc.vector.tensor_tensor(out=df[stage][:], in0=df[stage][:], in1=sc[stage][:], op=ALU.mult)
-            nc.vector.tensor_tensor(out=bi[stage][:], in0=df[stage][:], in1=q[:, 2, :], op=ALU.add)
+            nc.gpsimd.tensor_scalar(out=rs[stage][:], in0=q[:, 4, :], scalar1=EPS, scalar2=None, op0=ALU.add)
+            nc.gpsimd.tensor_tensor(out=rs[stage][:], in0=rs[stage][:], in1=mhalf[:, 0:8 * (stage + 1)], op=ALU.pow)
+            nc.gpsimd.tensor_tensor(out=sc[stage][:], in0=q[:, 1, :], in1=rs[stage][:], op=ALU.mult)
+            nc.gpsimd.tensor_tensor(out=df[stage][:], in0=q[:, 0, :], in1=q[:, 3, :], op=ALU.subtract)
+            nc.gpsimd.tensor_tensor(out=df[stage][:], in0=df[stage][:], in1=sc[stage][:], op=ALU.mult)
+            nc.gpsimd.tensor_tensor(out=bi[stage][:], in0=df[stage][:], in1=q[:, 2, :], op=ALU.add)
 
         def mm2(c, n, dg):
             for kk in range(4):
@@ -106,33 +112,33 @@ def tile_af_2_pa_t_kernel(tc, t, W1, b1, g1, beta1, m1, v1, W2, b2, g2, beta2, m
             rawp = ph1.enter_context(tc.tile_pool(name="rawp", bufs=3))
             wgrpp = ph1.enter_context(tc.tile_pool(name="wgrpp", bufs=4))
             ssp = ph1.enter_context(tc.tile_pool(name="ssp", bufs=2))
-            sgp = ph1.enter_context(tc.tile_pool(name="sgp", bufs=2))
+            sgp = ph1.enter_context(tc.tile_pool(name="sgp", bufs=3))
             swp = ph1.enter_context(tc.tile_pool(name="swp", bufs=2))
             hp = ph1.enter_context(tc.tile_pool(name="hp", bufs=3))
 
-            def load_w1(n):
-                raw = rawp.tile([P, 4096], BF16, name="wraw")
-                nc.sync.dma_start(out=raw.rearrange("p (u x) -> p u x", u=2), in_=W1[n].rearrange("(u p e) d -> p u (e d)", u=2, p=P, e=2))
-                live[("w1raw", n)] = raw
+            def load_w1(n, halves):
+                if ("w1raw", n) not in live:
+                    live[("w1raw", n)] = rawp.tile([P, 4096], BF16, name="wraw")
+                src = W1[n].rearrange("(u p e) d -> p u (e d)", u=2, p=P, e=2)
+                dst = live[("w1raw", n)].rearrange("p (u x) -> p u x", u=2)
+                nc.sync.dma_start(out=dst[:, halves], in_=src[:, halves])
 
             def load_w2(n):
                 raw = rawp.tile([P, 4096], BF16, name="wraw")
                 nc.sync.dma_start(out=raw.rearrange("p (k i) -> p k i", k=8), in_=W2[n].rearrange("(k p) i -> p k i", p=P))
                 live[("w2raw", n)] = raw
 
-            def w_run(kind, n):
-                for a in range(2):
-                    for b in range(2):
-                        bank = tp.tile([P, 2, 256], F32, name="tpb", tag="tp")
-                        for x in range(2):
-                            if kind == 1:
-                                words = live[("w1raw", n)][:, b * 2048 + x * 1024:b * 2048 + (x + 1) * 1024].bitcast(F32)[:, 256 * a:256 * a + 256]
-                            else:
-                                k = 4 * a + 2 * b + x
-                                words = live[("w2raw", n)][:, k * 512:(k + 1) * 512].bitcast(F32)
-                            for u in range(2):
-                                nc.tensor.transpose(bank[:, u, x * P:(x + 1) * P], words[:, u * P:(u + 1) * P], ident[:])
-                        live[("wbank", a, b)] = bank
+            def w_tr(kind, n, a, b):
+                bank = tp.tile([P, 2, 256], F32, name="tpb", tag="tp")
+                for x in range(2):
+                    if kind == 1:
+                        words = live[("w1raw", n)][:, b * 2048 + x * 1024:b * 2048 + (x + 1) * 1024].bitcast(F32)[:, 256 * a:256 * a + 256]
+                    else:
+                        k = 4 * a + 2 * b + x
+                        words = live[("w2raw", n)][:, k * 512:(k + 1) * 512].bitcast(F32)
+                    for u in range(2):
+                        nc.tensor.transpose(bank[:, u, x * P:(x + 1) * P], words[:, u * P:(u + 1) * P], ident[:])
+                live[("wbank", a, b)] = bank
 
             def w_evac(a, b, eng):
                 if b == 0:
@@ -144,155 +150,195 @@ def tile_af_2_pa_t_kernel(tc, t, W1, b1, g1, beta1, m1, v1, W2, b2, g2, beta2, m
                 else:
                     nc.vector.tensor_copy(out=dst, in_=src)
 
-            def w_quant(kind, n, a):
+            def w_quant(kind, n, a, b=None):
+                grp = live[("wgrp", a)]
+                lo, hi = (0, 512) if b is None else (256 * b, 256 * b + 256)
                 if kind == 1:
-                    cols = slice(n * 512, (n + 1) * 512)
-                    nc.vector.quantize_mx(out=w1w[:, a, cols].bitcast(FP8X4), scales=w1s[:, a, cols], in_=live[("wgrp", a)][:])
+                    cols = slice(n * 512 + lo, n * 512 + hi)
+                    nc.vector.quantize_mx(out=w1w[:, a, cols].bitcast(FP8X4), scales=w1s[:, a, cols], in_=grp[:, 4 * lo:4 * hi])
                 else:
-                    cols = slice(a * 512, (a + 1) * 512)
-                    nc.vector.quantize_mx(out=w2w[:, n, cols].bitcast(FP8X4), scales=w2s[:, n, cols], in_=live[("wgrp", a)][:])
+                    cols = slice(a * 512 + lo, a * 512 + hi)
+                    nc.vector.quantize_mx(out=w2w[:, n, cols].bitcast(FP8X4), scales=w2s[:, n, cols], in_=grp[:, 4 * lo:4 * hi])
 
-            def s_add(c, half):
-                if half == 0:
+            def s_add(c, bt0, nbt):
+                if bt0 == 0:
                     live[("s", c)] = ssp.tile([P, BT, DIM], BF16, name="s_sb")
-                rows = slice(2 * half, 2 * half + 2)
+                rows = slice(bt0, bt0 + nbt)
                 nc.vector.tensor_tensor(out=live[("s", c)][:, rows, :], in0=t_sb[c][:, rows, 0, :], in1=t_sb[c][:, rows, 1, :], op=ALU.add)
 
-            def t1_run(c, pairs):
-                for (g, half) in pairs:
+            def s_tr(c, half):
+                for g in range(2):
                     bank = tp.tile([P, 2, 256], F32, name="tpb", tag="tp")
                     for x in range(2):
                         words = live[("s", c)][:, 2 * half + x, :].bitcast(F32)
                         for u in range(2):
                             nc.tensor.transpose(bank[:, u, x * P:(x + 1) * P], words[:, 256 * g + u * P:256 * g + (u + 1) * P], ident[:])
-                    live[("tbank", g, half)] = bank
+                    live[("tbank", c, g, half)] = bank
 
-            def e1(c, g, half):
-                if ("sg", c, g) not in live:
-                    live[("sg", c, g)] = sgp.tile([P, 2048], BF16, name="sg", align_bytes=64)
-                dst = live[("sg", c, g)].bitcast(F32).rearrange("p (b u) -> p b u", u=2)[:, half * 256:(half + 1) * 256, :]
-                nc.scalar.copy(out=dst, in_=live[("tbank", g, half)].rearrange("p u b -> p b u"))
+            def s_evac(c, half, engs):
+                for g in range(2):
+                    if ("sg", c, g) not in live:
+                        live[("sg", c, g)] = sgp.tile([P, 2048], BF16, name="sg", align_bytes=64)
+                    dst = live[("sg", c, g)].bitcast(F32).rearrange("p (b u) -> p b u", u=2)[:, half * 256:(half + 1) * 256, :]
+                    src = live[("tbank", c, g, half)].rearrange("p u b -> p b u")
+                    if engs[g] == "S":
+                        nc.scalar.copy(out=dst, in_=src)
+                    else:
+                        nc.vector.tensor_copy(out=dst, in_=src)
 
-            def q1(c, g):
+            def s_quant(c, half=None):
                 if ("sw", c) not in live:
                     live[("sw", c)] = swp.tile([P, 2, CH], U32, name="sw", align_bytes=64)
                     live[("ss", c)] = swp.tile([P, 2, CH], U8, name="ss", align_bytes=64)
-                nc.vector.quantize_mx(out=live[("sw", c)][:, g, :].bitcast(FP8X4), scales=live[("ss", c)][:, g, :], in_=live[("sg", c, g)][:])
+                lo, hi = (0, 512) if half is None else (256 * half, 256 * half + 256)
+                for g in range(2):
+                    nc.vector.quantize_mx(out=live[("sw", c)][:, g, lo:hi].bitcast(FP8X4), scales=live[("ss", c)][:, g, lo:hi], in_=live[("sg", c, g)][:, 4 * lo:4 * hi])
 
-            def mm1(j):
-                c, n = j // 2, j % 2
-                for tt in range(4):
-                    acc = mp.tile([P, CH], F32, name="acc", tag="mp")
+            def mm1(c, n, half=None, tts=(0, 1, 2, 3)):
+                lo, hi = (0, 512) if half is None else (256 * half, 256 * half + 256)
+                for tt in tts:
+                    acc = mp.tile([P, hi - lo], F32, name="acc", tag="mp")
                     cols = slice(n * 512 + tt * P, n * 512 + (tt + 1) * P)
                     for g in range(2):
                         nc.tensor.matmul_mx(out=acc[:], lhsT=w1w[:, g, cols].bitcast(FP8X4), lhsT_scale=w1s[:, g, cols],
-                                            rhs=live[("sw", c)][:, g, :].bitcast(FP8X4), rhs_scale=live[("ss", c)][:, g, :],
+                                            rhs=live[("sw", c)][:, g, lo:hi].bitcast(FP8X4), rhs_scale=live[("ss", c)][:, g, lo:hi],
                                             start=(g == 0), stop=(g == 1))
                     live[("acc1", tt)] = acc
 
-            def relu(j):
-                n = j % 2
-                hT = hp.tile([P, 4, CH], BF16, name="hT")
-                for tt in range(4):
+            def relu(c, n, half=None, tts=(0, 1, 2, 3)):
+                lo, hi = (0, 512) if half is None else (256 * half, 256 * half + 256)
+                if ("hT", c, n) not in live:
+                    live[("hT", c, n)] = hp.tile([P, 4, CH], BF16, name="hT")
+                for tt in tts:
                     col = (tt % 2) * 4 + 2 * n + tt // 2
-                    nc.scalar.activation(out=hT[:, tt, :], in_=live[("acc1", tt)][:], func=ACT.Relu,
+                    nc.scalar.activation(out=live[("hT", c, n)][:, tt, lo:hi], in_=live[("acc1", tt)][:], func=ACT.Relu,
                                          bias=bi[0][:, col:col + 1], scale=sc[0][:, col:col + 1])
-                live[("hT", j)] = hT
 
             def rg(j):
                 hg = hp.tile([P, 4 * CH], BF16, name="hg", align_bytes=64)
-                nc.vector.tensor_copy(out=hg.rearrange("p (c i t) -> p c t i", i=4, t=4), in_=live[("hT", j)].rearrange("p t (c i) -> p c t i", i=4))
+                nc.vector.tensor_copy(out=hg.rearrange("p (c i t) -> p c t i", i=4, t=4), in_=live[("hT", j // 2, j % 2)].rearrange("p t (c i) -> p c t i", i=4))
                 live[("hg", j)] = hg
 
             def q2(j):
                 nc.vector.quantize_mx(out=hw[:, j, :].bitcast(FP8X4), scales=hs[:, j, :], in_=live[("hg", j)][:])
 
+            nc.vector.memset(dummy[:], 0.0)
+            nc.scalar.activation(out=dummy[:], in_=dummy[:], func=ACT.Sigmoid)
             make_identity(nc, ident[:])
             nc.vector.memset(x1[:], 0.0)
             nc.vector.memset(x2[:], 0.0)
-            for v, vec in enumerate((b1, g1, beta1, m1, v1)):
-                nc.scalar.dma_start(out=x1[4 * v:4 * v + 4, :], in_=vec.rearrange("n (u c) -> (n u) c", c=256))
-            load_t(0, 2)
-            load_w1(0)
-            load_w1(1)
-            load_t(1, 2)
-            load_t(2, 1)
-            load_t(3, 1)
+            nc.vector.memset(mhalf[:], -0.5)
+            load_w1(0, slice(0, 1))
+            load_t(0, 0, 1)
+            load_t(0, 1, 1)
+            load_w1(0, slice(1, 2))
+            load_params(0)
+            load_t(0, 2, 1)
+            load_t(0, 3, 1)
+            load_w1(1, slice(0, 2))
+            for bt in range(BT):
+                load_t(1, bt, 1)
+            load_t(2, 0, 2)
+            load_params(1)
+            load_t(2, 2, 2)
             load_w2(0)
+            load_t(3, 0, 2)
+            load_t(3, 2, 2)
+            w_tr(1, 0, 0, 0)
+            w_tr(1, 0, 1, 0)
+            w_evac(0, 0, "S")
+            w_evac(1, 0, "S")
+            s_add(0, 0, 1)
+            w_quant(1, 0, 0, 0)
+            w_quant(1, 0, 1, 0)
+            s_add(0, 1, 1)
+            s_tr(0, 0)
+            w_tr(1, 0, 0, 1)
+            w_tr(1, 0, 1, 1)
+            load_w2(1)
+            s_evac(0, 0, "SS")
+            w_evac(0, 1, "S")
+            w_evac(1, 1, "S")
+            s_add(0, 2, 1)
             params_cast(0)
-            for half in range(2):
-                s_add(0, half)
-                t1_run(0, [(0, half), (1, half)])
-                for g in range(2):
-                    e1(0, g, half)
-                if half == 0:
-                    params_pe(0)
-            q1(0, 0)
-            q1(0, 1)
-            for n in range(2):
-                w_run(1, n)
-                for a in range(2):
-                    for b in range(2):
-                        w_evac(a, b, "V" if (a, b) == (1, 1) else "S")
-                w_quant(1, n, 0)
-                w_quant(1, n, 1)
-                if n == 0:
-                    load_w2(1)
-                    for v, vec in enumerate((b2, g2, beta2, m2, v2)):
-                        nc.sync.dma_start(out=x2[16 * v:16 * v + 16, :], in_=vec.rearrange("n (k c) -> (n k) c", c=P))
-            for j in range(2 * NCH):
+            params_pe(0)
+            s_quant(0, 0)
+            s_add(0, 3, 1)
+            w_quant(1, 0, 0, 1)
+            w_quant(1, 0, 1, 1)
+            mm1(0, 0, 0, (0, 1))
+            s_tr(0, 1)
+            mm1(0, 0, 0, (2, 3))
+            relu(0, 0, 0, (0, 1))
+            s_evac(0, 1, "SS")
+            relu(0, 0, 0, (2, 3))
+            s_quant(0, 1)
+            for a in range(2):
+                for b in range(2):
+                    w_tr(1, 1, a, b)
+            mm1(0, 0, 1)
+            w_evac(0, 0, "S")
+            w_evac(0, 1, "S")
+            s_add(1, 0, 1)
+            w_quant(1, 1, 0)
+            w_evac(1, 0, "S")
+            w_evac(1, 1, "S")
+            s_add(1, 1, 1)
+            w_quant(1, 1, 1)
+            relu(0, 0, 1)
+            s_tr(1, 0)
+            mm1(0, 1, None, (0, 1))
+            s_evac(1, 0, "SS")
+            s_add(1, 2, 1)
+            s_add(1, 3, 1)
+            s_tr(1, 1)
+            rg(0)
+            mm1(0, 1, None, (2, 3))
+            relu(0, 1, None, (0, 1))
+            s_evac(1, 1, "SS")
+            relu(0, 1, None, (2, 3))
+            s_add(2, 0, 2)
+            s_quant(1)
+            q2(0)
+            for j in range(2, 2 * NCH):
                 c, n = j // 2, j % 2
-                if j < 2:
-                    mm1(j)
-                    s_add(1, j)
-                    t1_run(1, [(0, j), (1, j)])
-                    relu(j)
-                    for g in range(2):
-                        e1(1, g, j)
-                    if j == 1:
-                        rg(0)
-                        q1(1, 0)
-                        q1(1, 1)
-                        q2(0)
-                        for half in range(2):
-                            s_add(2, half)
-                elif j < 6:
-                    t1_run(c + 1, [(n, 0), (n, 1)])
-                    mm1(j)
-                    for half in range(2):
-                        e1(c + 1, n, half)
-                    relu(j)
-                    rg(j - 1)
-                    if n == 1:
-                        q1(c + 1, 0)
-                    q2(j - 1)
-                    if n == 1:
-                        q1(c + 1, 1)
-                        if j == 3:
-                            for half in range(2):
-                                s_add(3, half)
+                if c < NCH - 1:
+                    s_tr(c + 1, n)
+                    mm1(c, n)
+                    s_evac(c + 1, n, "SS")
+                    relu(c, n)
+                    if n == 0:
+                        rg(j - 1)
+                        s_add(c + 1, 2, 2)
+                        q2(j - 1)
+                    else:
+                        if c + 2 < NCH:
+                            s_add(c + 2, 0, 2)
+                        rg(j - 1)
+                        s_quant(c + 1)
+                        q2(j - 1)
                 else:
-                    w_run(2, j - 6)
-                    mm1(j)
+                    for a in range(2):
+                        for b in range(2):
+                            w_tr(2, n, a, b)
+                    mm1(c, n)
                     w_evac(0, 0, "S")
                     w_evac(1, 0, "S")
-                    relu(j)
-                    w_evac(0, 1, "V")
-                    w_evac(1, 1, "V")
-                    if j == 6:
+                    if n == 0:
                         params_cast(1)
-                    w_quant(2, j - 6, 0)
-                    w_quant(2, j - 6, 1)
-                    if j == 6:
+                    w_evac(0, 1, "S")
+                    w_evac(1, 1, "V")
+                    relu(c, n)
+                    rg(j - 1)
+                    w_quant(2, n, 0)
+                    w_quant(2, n, 1)
+                    if n == 0:
                         params_pe(1)
+                    q2(j - 1)
             for k in range(LAG):
                 mm2(*units[k])
                 sig(*units[k])
-            rg(5)
-            rg(6)
-            q2(5)
             rg(7)
-            q2(6)
             q2(7)
 
         with ExitStack() as ph2:
@@ -320,9 +366,7 @@ def tile_af_2_pa_t_kernel(tc, t, W1, b1, g1, beta1, m1, v1, W2, b2, g2, beta2, m
                 o = live["o"]
                 p1 = live["p1"]
                 if eng == "G":
-                    for x in range(GP):
-                        cols = slice(x * (CH // GP), (x + 1) * (CH // GP))
-                        nc.gpsimd.tensor_tensor(out=o[:, bt, cols], in0=o[:, bt, cols], in1=p1[:, bt, cols], op=ALU.add)
+                    nc.gpsimd.tensor_tensor(out=o[:, bt, :], in0=o[:, bt, :], in1=p1[:, bt, :], op=ALU.add)
                 else:
                     nc.vector.tensor_tensor(out=o[:, bt, :], in0=o[:, bt, :], in1=p1[:, bt, :], op=ALU.add)
 
@@ -330,24 +374,22 @@ def tile_af_2_pa_t_kernel(tc, t, W1, b1, g1, beta1, m1, v1, W2, b2, g2, beta2, m
                 nc.sync.dma_start(out=out_v[:, c * BT + bt0:c * BT + bt0 + nbt, dg * CH:(dg + 1) * CH], in_=live["o"][:, bt0:bt0 + nbt, :])
 
             for k in range(LAG, len(units) + LAG):
-                if k >= LAG:
-                    t2(*units[k - LAG])
+                t2(*units[k - LAG])
                 if k < len(units):
                     mm2(*units[k])
                     sig(*units[k])
-                if k >= LAG:
-                    c, n, dg = units[k - LAG]
-                    last = k == len(units) + LAG - 1
+                c, n, dg = units[k - LAG]
+                last = k == len(units) + LAG - 1
+                for bt in range(BT):
+                    prod(c, n, dg, bt)
+                    if last and bt < 2:
+                        add(bt, "G")
+                if last:
+                    store(c, dg, 0, 2)
+                    add(2, "V")
+                    add(3, "V")
+                    store(c, dg, 2, 2)
+                if n == 1 and not last:
                     for bt in range(BT):
-                        prod(c, n, dg, bt)
-                        if last and bt < 2:
-                            add(bt, "G")
-                    if last:
-                        store(c, dg, 0, 2)
-                        add(2, "V")
-                        add(3, "V")
-                        store(c, dg, 2, 2)
-                    if n == 1 and not last:
-                        for bt in range(BT):
-                            add(bt, "G")
-                        store(c, dg, 0, BT)
+                        add(bt, "G")
+                    store(c, dg, 0, BT)

@@ -62,7 +62,7 @@ def tile_af_2_pa_t_kernel(tc, t, W1, b1, g1, beta1, m1, v1, W2, b2, g2, beta2, m
             vecs = ((b1, g1, beta1, m1, v1), (b2, g2, beta2, m2, v2))[stage]
             for v, vec in enumerate(vecs):
                 if stage == 0:
-                    nc.sync.dma_start(out=x1[4 * v:4 * v + 4, :], in_=vec.rearrange("n (u c) -> (n u) c", c=256))
+                    nc.scalar.dma_start(out=x1[4 * v:4 * v + 4, :], in_=vec.rearrange("n (u c) -> (n u) c", c=256))
                 else:
                     nc.sync.dma_start(out=x2[16 * v:16 * v + 16, :], in_=vec.rearrange("n (k c) -> (n k) c", c=P))
 
@@ -222,24 +222,25 @@ def tile_af_2_pa_t_kernel(tc, t, W1, b1, g1, beta1, m1, v1, W2, b2, g2, beta2, m
             def q2(j):
                 nc.vector.quantize_mx(out=hw[:, j, :].bitcast(FP8X4), scales=hs[:, j, :], in_=live[("hg", j)][:])
 
-            nc.vector.memset(dummy[:], 0.0)
-            nc.scalar.activation(out=dummy[:], in_=dummy[:], func=ACT.Sigmoid)
-            make_identity(nc, ident[:])
             nc.vector.memset(x1[:], 0.0)
+            nc.vector.memset(dummy[:], 0.0)
             nc.vector.memset(x2[:], 0.0)
             nc.vector.memset(mhalf[:], -0.5)
+            load_params(0)
+            nc.scalar.activation(out=dummy[:], in_=dummy[:], func=ACT.Sigmoid)
+            make_identity(nc, ident[:])
             load_w1(0, slice(0, 1))
             load_t(0, 0, 1)
             load_t(0, 1, 1)
             load_w1(0, slice(1, 2))
-            load_params(0)
             load_t(0, 2, 1)
             load_t(0, 3, 1)
             load_w1(1, slice(0, 2))
-            for bt in range(BT):
+            load_t(1, 0, 1)
+            load_params(1)
+            for bt in range(1, BT):
                 load_t(1, bt, 1)
             load_t(2, 0, 2)
-            load_params(1)
             load_t(2, 2, 2)
             load_w2(0)
             load_t(3, 0, 2)
@@ -248,6 +249,8 @@ def tile_af_2_pa_t_kernel(tc, t, W1, b1, g1, beta1, m1, v1, W2, b2, g2, beta2, m
             w_tr(1, 0, 1, 0)
             w_evac(0, 0, "S")
             w_evac(1, 0, "S")
+            params_cast(0)
+            params_pe(0)
             s_add(0, 0, 1)
             w_quant(1, 0, 0, 0)
             w_quant(1, 0, 1, 0)
@@ -260,8 +263,6 @@ def tile_af_2_pa_t_kernel(tc, t, W1, b1, g1, beta1, m1, v1, W2, b2, g2, beta2, m
             w_evac(0, 1, "S")
             w_evac(1, 1, "S")
             s_add(0, 2, 1)
-            params_cast(0)
-            params_pe(0)
             s_quant(0, 0)
             s_add(0, 3, 1)
             w_quant(1, 0, 0, 1)
@@ -297,6 +298,8 @@ def tile_af_2_pa_t_kernel(tc, t, W1, b1, g1, beta1, m1, v1, W2, b2, g2, beta2, m
             relu(0, 1, None, (0, 1))
             s_evac(1, 1, "SS")
             relu(0, 1, None, (2, 3))
+            params_cast(1)
+            params_pe(1)
             s_add(2, 0, 2)
             s_quant(1)
             q2(0)
@@ -318,24 +321,23 @@ def tile_af_2_pa_t_kernel(tc, t, W1, b1, g1, beta1, m1, v1, W2, b2, g2, beta2, m
                         s_quant(c + 1)
                         q2(j - 1)
                 else:
+                    if n == 1:
+                        mm2(*units[0])
+                        sig(*units[0])
                     for a in range(2):
                         for b in range(2):
                             w_tr(2, n, a, b)
                     mm1(c, n)
                     w_evac(0, 0, "S")
                     w_evac(1, 0, "S")
-                    if n == 0:
-                        params_cast(1)
                     w_evac(0, 1, "S")
                     w_evac(1, 1, "V")
                     relu(c, n)
                     rg(j - 1)
                     w_quant(2, n, 0)
                     w_quant(2, n, 1)
-                    if n == 0:
-                        params_pe(1)
                     q2(j - 1)
-            for k in range(LAG):
+            for k in range(1, LAG):
                 mm2(*units[k])
                 sig(*units[k])
             rg(7)

@@ -45,7 +45,6 @@ def tile_af_2_pa_t_kernel(tc, t, W1, b1, g1, beta1, m1, v1, W2, b2, g2, beta2, m
         x2 = const.tile([P, P], BF16, name="x2")
         xf1 = const.tile([P, 2, P], F32, name="xf1")
         xf2 = const.tile([P, P], F32, name="xf2")
-        mhalf = const.tile([P, 16], F32, name="mhalf")
         dummy = const.tile([P, 1], F32, name="dummy")
         pr = [const.tile([P, 5, 8], F32, name="pr1"), const.tile([P, 5, 16], F32, name="pr2")]
         sc = [const.tile([P, 8], F32, name="sc1"), const.tile([P, 16], F32, name="sc2")]
@@ -59,36 +58,41 @@ def tile_af_2_pa_t_kernel(tc, t, W1, b1, g1, beta1, m1, v1, W2, b2, g2, beta2, m
             nc.sync.dma_start(out=t_sb[c][:, bt0:bt0 + nbt], in_=t_v[:, c * BT + bt0:c * BT + bt0 + nbt])
 
         def load_params(stage):
-            vecs = ((b1, g1, beta1, m1, v1), (b2, g2, beta2, m2, v2))[stage]
+            vecs = ((v1, b1, g1, beta1, m1), (v2, b2, g2, beta2, m2))[stage]
             for v, vec in enumerate(vecs):
                 if stage == 0:
-                    nc.scalar.dma_start(out=x1[4 * v:4 * v + 4, :], in_=vec.rearrange("n (u c) -> (n u) c", c=256))
+                    nc.sync.dma_start(out=x1[4 * v:4 * v + 4, :], in_=vec.rearrange("n (u c) -> (n u) c", c=256))
                 else:
-                    nc.sync.dma_start(out=x2[16 * v:16 * v + 16, :], in_=vec.rearrange("n (k c) -> (n k) c", c=P))
+                    nc.scalar.dma_start(out=x2[16 * v:16 * v + 16, :], in_=vec.rearrange("n (k c) -> (n k) c", c=P))
 
         def params_cast(stage):
-            if stage == 0:
-                nc.gpsimd.tensor_copy(out=xf1[:], in_=x1.rearrange("r (p e) -> r e p", e=2))
-            else:
-                nc.gpsimd.tensor_copy(out=xf2[:], in_=x2[:])
+            x, xf = ((x1.rearrange("r (p e) -> r e p", e=2), xf1), (x2, xf2))[stage]
+            nv = (4, 16)[stage]
+            nc.gpsimd.tensor_scalar(out=xf[:], in0=x[:], scalar1=1.0, scalar2=0.0, op0=ALU.mult, op1=ALU.add)
+            nc.gpsimd.tensor_scalar(out=xf[0:nv], in0=xf[0:nv], scalar1=1.0, scalar2=EPS, op0=ALU.mult, op1=ALU.add)
+            nc.scalar.sqrt(out=xf[0:nv], in_=xf[0:nv])
 
-        def params_pe(stage):
+        def params_tr(stage):
+            bank = tp.tile([P, 2, P], F32, name="tpb", tag="tp")
             if stage == 0:
-                bank = tp.tile([P, 2, P], F32, name="tpb", tag="tp")
                 for e in range(2):
                     nc.tensor.transpose(bank[:, e, :], xf1[:, e, :], ident[:])
+            else:
+                nc.tensor.transpose(bank[:, 0, :], xf2[:], ident[:])
+            live["pbank"] = bank
+
+        def params_out(stage):
+            bank = live["pbank"]
+            if stage == 0:
                 nc.vector.tensor_copy(out=pr[0].rearrange("p v (e j) -> p v e j", e=2), in_=bank[:, :, 0:20].rearrange("p e (v j) -> p v e j", v=5))
             else:
-                bank = tp.tile([P, P], F32, name="tpb", tag="tp")
-                nc.tensor.transpose(bank[:], xf2[:], ident[:])
-                nc.vector.tensor_copy(out=pr[1][:], in_=bank[:, 0:80].rearrange("p (v j) -> p v j", v=5))
+                nc.vector.tensor_copy(out=pr[1][:], in_=bank[:, 0, 0:80].rearrange("p (v j) -> p v j", v=5))
             q = pr[stage]
-            nc.gpsimd.tensor_scalar(out=rs[stage][:], in0=q[:, 4, :], scalar1=EPS, scalar2=None, op0=ALU.add)
-            nc.gpsimd.tensor_tensor(out=rs[stage][:], in0=rs[stage][:], in1=mhalf[:, 0:8 * (stage + 1)], op=ALU.pow)
-            nc.gpsimd.tensor_tensor(out=sc[stage][:], in0=q[:, 1, :], in1=rs[stage][:], op=ALU.mult)
-            nc.gpsimd.tensor_tensor(out=df[stage][:], in0=q[:, 0, :], in1=q[:, 3, :], op=ALU.subtract)
+            nc.vector.reciprocal(out=rs[stage][:], in_=q[:, 0, :])
+            nc.gpsimd.tensor_tensor(out=df[stage][:], in0=q[:, 1, :], in1=q[:, 4, :], op=ALU.subtract)
+            nc.gpsimd.tensor_tensor(out=sc[stage][:], in0=q[:, 2, :], in1=rs[stage][:], op=ALU.mult)
             nc.gpsimd.tensor_tensor(out=df[stage][:], in0=df[stage][:], in1=sc[stage][:], op=ALU.mult)
-            nc.gpsimd.tensor_tensor(out=bi[stage][:], in0=df[stage][:], in1=q[:, 2, :], op=ALU.add)
+            nc.gpsimd.tensor_tensor(out=bi[stage][:], in0=df[stage][:], in1=q[:, 3, :], op=ALU.add)
 
         def mm2(c, n, dg):
             for kk in range(4):
@@ -222,23 +226,21 @@ def tile_af_2_pa_t_kernel(tc, t, W1, b1, g1, beta1, m1, v1, W2, b2, g2, beta2, m
             def q2(j):
                 nc.vector.quantize_mx(out=hw[:, j, :].bitcast(FP8X4), scales=hs[:, j, :], in_=live[("hg", j)][:])
 
+            nc.vector.memset(x2[:], 0.0)
             nc.vector.memset(x1[:], 0.0)
             nc.vector.memset(dummy[:], 0.0)
-            nc.vector.memset(x2[:], 0.0)
-            nc.vector.memset(mhalf[:], -0.5)
-            load_params(0)
-            nc.scalar.activation(out=dummy[:], in_=dummy[:], func=ACT.Sigmoid)
+            load_params(1)
+            nc.scalar.sqrt(out=dummy[:], in_=dummy[:])
             make_identity(nc, ident[:])
             load_w1(0, slice(0, 1))
+            load_params(0)
             load_t(0, 0, 1)
             load_t(0, 1, 1)
             load_w1(0, slice(1, 2))
             load_t(0, 2, 1)
             load_t(0, 3, 1)
             load_w1(1, slice(0, 2))
-            load_t(1, 0, 1)
-            load_params(1)
-            for bt in range(1, BT):
+            for bt in range(BT):
                 load_t(1, bt, 1)
             load_t(2, 0, 2)
             load_t(2, 2, 2)
@@ -250,11 +252,14 @@ def tile_af_2_pa_t_kernel(tc, t, W1, b1, g1, beta1, m1, v1, W2, b2, g2, beta2, m
             w_evac(0, 0, "S")
             w_evac(1, 0, "S")
             params_cast(0)
-            params_pe(0)
+            params_cast(1)
+            nc.scalar.activation(out=dummy[:], in_=dummy[:], func=ACT.Sigmoid)
             s_add(0, 0, 1)
             w_quant(1, 0, 0, 0)
             w_quant(1, 0, 1, 0)
+            params_tr(0)
             s_add(0, 1, 1)
+            params_out(0)
             s_tr(0, 0)
             w_tr(1, 0, 0, 1)
             w_tr(1, 0, 1, 1)
@@ -293,54 +298,53 @@ def tile_af_2_pa_t_kernel(tc, t, W1, b1, g1, beta1, m1, v1, W2, b2, g2, beta2, m
             s_add(1, 2, 1)
             s_add(1, 3, 1)
             s_tr(1, 1)
+            params_tr(1)
             rg(0)
             mm1(0, 1, None, (2, 3))
             relu(0, 1, None, (0, 1))
             s_evac(1, 1, "SS")
             relu(0, 1, None, (2, 3))
-            params_cast(1)
-            params_pe(1)
-            s_add(2, 0, 2)
             s_quant(1)
+            s_add(2, 0, 2)
             q2(0)
-            for j in range(2, 2 * NCH):
-                c, n = j // 2, j % 2
+            params_out(1)
+            for c in range(1, NCH):
+                mm1(c, 0)
+                relu(c, 0)
                 if c < NCH - 1:
-                    s_tr(c + 1, n)
-                    mm1(c, n)
-                    s_evac(c + 1, n, "SS")
-                    relu(c, n)
-                    if n == 0:
-                        rg(j - 1)
-                        s_add(c + 1, 2, 2)
-                        q2(j - 1)
-                    else:
-                        if c + 2 < NCH:
-                            s_add(c + 2, 0, 2)
-                        rg(j - 1)
-                        s_quant(c + 1)
-                        q2(j - 1)
+                    if c > 1:
+                        s_add(c + 1, 0, 2)
+                    rg(2 * c - 1)
+                    s_add(c + 1, 2, 2)
+                    s_tr(c + 1, 0)
+                    s_evac(c + 1, 0, "SS")
+                    s_tr(c + 1, 1)
+                    s_evac(c + 1, 1, "SS")
+                    q2(2 * c - 1)
+                    rg(2 * c)
+                    s_quant(c + 1)
+                    q2(2 * c)
+                    mm1(c, 1)
+                    relu(c, 1)
                 else:
-                    if n == 1:
-                        mm2(*units[0])
-                        sig(*units[0])
-                    for a in range(2):
-                        for b in range(2):
-                            w_tr(2, n, a, b)
-                    mm1(c, n)
-                    w_evac(0, 0, "S")
-                    w_evac(1, 0, "S")
-                    w_evac(0, 1, "S")
-                    w_evac(1, 1, "V")
-                    relu(c, n)
-                    rg(j - 1)
-                    w_quant(2, n, 0)
-                    w_quant(2, n, 1)
-                    q2(j - 1)
-            for k in range(1, LAG):
-                mm2(*units[k])
-                sig(*units[k])
-            rg(7)
+                    rg(2 * c - 1)
+                    for n in range(NB):
+                        for a in range(2):
+                            for b in range(2):
+                                w_tr(2, n, a, b)
+                        for a in range(2):
+                            for b in range(2):
+                                w_evac(a, b, "V" if b == 1 else "S")
+                        q2(2 * c - 1 + n)
+                        w_quant(2, n, 0)
+                        w_quant(2, n, 1)
+                        rg(2 * c + n)
+                        if n == 0:
+                            mm1(c, 1)
+                            relu(c, 1)
+                    for n in range(NB):
+                        mm2(*units[n])
+                        sig(*units[n])
             q2(7)
 
         with ExitStack() as ph2:
@@ -387,10 +391,10 @@ def tile_af_2_pa_t_kernel(tc, t, W1, b1, g1, beta1, m1, v1, W2, b2, g2, beta2, m
                     if last and bt < 2:
                         add(bt, "G")
                 if last:
-                    store(c, dg, 0, 2)
                     add(2, "V")
                     add(3, "V")
-                    store(c, dg, 2, 2)
+                    for bt in range(BT):
+                        store(c, dg, bt, 1)
                 if n == 1 and not last:
                     for bt in range(BT):
                         add(bt, "G")

@@ -43,8 +43,13 @@ def tile_af_2_pa_t_kernel(tc, t, W1, b1, g1, beta1, m1, v1, W2, b2, g2, beta2, m
         t_sb = [const.tile([P, BT, NB, DIM], BF16, name="t_sb%d" % c) for c in range(NCH)]
         x1 = const.tile([P, 256], BF16, name="x1")
         x2 = const.tile([P, P], BF16, name="x2")
+        v1r = const.tile([4, 256], BF16, name="v1r")
+        v2r = const.tile([16, P], BF16, name="v2r")
+        xv1 = const.tile([4, 2, P], F32, name="xv1")
+        xv2 = const.tile([16, P], F32, name="xv2")
         xf1 = const.tile([P, 2, P], F32, name="xf1")
         xf2 = const.tile([P, P], F32, name="xf2")
+        zb = const.tile([P, CH], BF16, name="zb")
         dummy = const.tile([P, 1], F32, name="dummy")
         pr = [const.tile([P, 5, 8], F32, name="pr1"), const.tile([P, 5, 16], F32, name="pr2")]
         sc = [const.tile([P, 8], F32, name="sc1"), const.tile([P, 16], F32, name="sc2")]
@@ -57,20 +62,24 @@ def tile_af_2_pa_t_kernel(tc, t, W1, b1, g1, beta1, m1, v1, W2, b2, g2, beta2, m
         def load_t(c, bt0, nbt):
             nc.sync.dma_start(out=t_sb[c][:, bt0:bt0 + nbt], in_=t_v[:, c * BT + bt0:c * BT + bt0 + nbt])
 
-        def load_params(stage):
+        def load_params(stage, which):
             vecs = ((v1, b1, g1, beta1, m1), (v2, b2, g2, beta2, m2))[stage]
-            for v, vec in enumerate(vecs):
+            for v in which:
+                vec = vecs[v]
                 if stage == 0:
-                    nc.sync.dma_start(out=x1[4 * v:4 * v + 4, :], in_=vec.rearrange("n (u c) -> (n u) c", c=256))
+                    nc.sync.dma_start(out=v1r[:] if v == 0 else x1[4 * v:4 * v + 4, :], in_=vec.rearrange("n (u c) -> (n u) c", c=256))
                 else:
-                    nc.scalar.dma_start(out=x2[16 * v:16 * v + 16, :], in_=vec.rearrange("n (k c) -> (n k) c", c=P))
+                    nc.sync.dma_start(out=v2r[:] if v == 0 else x2[16 * v:16 * v + 16, :], in_=vec.rearrange("n (k c) -> (n k) c", c=P))
+
+        def params_sqrt(stage):
+            x, xv = ((v1r.rearrange("r (p e) -> r e p", e=2), xv1), (v2r, xv2))[stage]
+            nc.vector.tensor_scalar(out=xv[:], in0=x[:], scalar1=1.0, scalar2=EPS, op0=ALU.mult, op1=ALU.add)
+            nc.scalar.sqrt(out=xv[:], in_=xv[:])
 
         def params_cast(stage):
-            x, xf = ((x1.rearrange("r (p e) -> r e p", e=2), xf1), (x2, xf2))[stage]
-            nv = (4, 16)[stage]
+            x, xf, xv, nv = ((x1.rearrange("r (p e) -> r e p", e=2), xf1, xv1, 4), (x2, xf2, xv2, 16))[stage]
             nc.gpsimd.tensor_scalar(out=xf[:], in0=x[:], scalar1=1.0, scalar2=0.0, op0=ALU.mult, op1=ALU.add)
-            nc.gpsimd.tensor_scalar(out=xf[0:nv], in0=xf[0:nv], scalar1=1.0, scalar2=EPS, op0=ALU.mult, op1=ALU.add)
-            nc.scalar.sqrt(out=xf[0:nv], in_=xf[0:nv])
+            nc.gpsimd.tensor_scalar(out=xf[0:nv], in0=xv[:], scalar1=1.0, scalar2=0.0, op0=ALU.mult, op1=ALU.add)
 
         def params_tr(stage):
             bank = tp.tile([P, 2, P], F32, name="tpb", tag="tp")
@@ -226,15 +235,22 @@ def tile_af_2_pa_t_kernel(tc, t, W1, b1, g1, beta1, m1, v1, W2, b2, g2, beta2, m
             def q2(j):
                 nc.vector.quantize_mx(out=hw[:, j, :].bitcast(FP8X4), scales=hs[:, j, :], in_=live[("hg", j)][:])
 
-            nc.vector.memset(x2[:], 0.0)
+            def warm(count):
+                acc = mp.tile([P, CH], F32, name="acc", tag="mp")
+                for i in range(count):
+                    nc.tensor.matmul(out=acc[:], lhsT=zb[:, 0:P], rhs=zb[:], start=True, stop=True)
+
+            nc.vector.memset(zb[:], 0.0)
             nc.vector.memset(x1[:], 0.0)
             nc.vector.memset(dummy[:], 0.0)
-            load_params(1)
+            nc.vector.memset(x2[:], 0.0)
             nc.scalar.sqrt(out=dummy[:], in_=dummy[:])
             make_identity(nc, ident[:])
             load_w1(0, slice(0, 1))
-            load_params(0)
+            load_params(0, (0,))
+            load_params(1, (0,))
             load_t(0, 0, 1)
+            load_params(0, (1, 2, 3, 4))
             load_t(0, 1, 1)
             load_w1(0, slice(1, 2))
             load_t(0, 2, 1)
@@ -242,29 +258,35 @@ def tile_af_2_pa_t_kernel(tc, t, W1, b1, g1, beta1, m1, v1, W2, b2, g2, beta2, m
             load_w1(1, slice(0, 2))
             for bt in range(BT):
                 load_t(1, bt, 1)
+            load_params(1, (1, 2, 3, 4))
             load_t(2, 0, 2)
             load_t(2, 2, 2)
             load_w2(0)
             load_t(3, 0, 2)
             load_t(3, 2, 2)
+            warm(5)
             w_tr(1, 0, 0, 0)
             w_tr(1, 0, 1, 0)
+            warm(3)
             w_evac(0, 0, "S")
             w_evac(1, 0, "S")
-            params_cast(0)
-            params_cast(1)
+            params_sqrt(0)
+            params_sqrt(1)
             nc.scalar.activation(out=dummy[:], in_=dummy[:], func=ACT.Sigmoid)
             s_add(0, 0, 1)
             w_quant(1, 0, 0, 0)
             w_quant(1, 0, 1, 0)
+            params_cast(0)
             params_tr(0)
+            warm(2)
             s_add(0, 1, 1)
             params_out(0)
             s_tr(0, 0)
+            s_evac(0, 0, "SS")
             w_tr(1, 0, 0, 1)
             w_tr(1, 0, 1, 1)
+            warm(3)
             load_w2(1)
-            s_evac(0, 0, "SS")
             w_evac(0, 1, "S")
             w_evac(1, 1, "S")
             s_add(0, 2, 1)
@@ -276,14 +298,14 @@ def tile_af_2_pa_t_kernel(tc, t, W1, b1, g1, beta1, m1, v1, W2, b2, g2, beta2, m
             s_tr(0, 1)
             mm1(0, 0, 0, (2, 3))
             relu(0, 0, 0, (0, 1))
-            s_evac(0, 1, "SS")
+            s_evac(0, 1, "VS")
             relu(0, 0, 0, (2, 3))
             s_quant(0, 1)
             for a in range(2):
                 for b in range(2):
                     w_tr(1, 1, a, b)
             mm1(0, 0, 1)
-            w_evac(0, 0, "S")
+            w_evac(0, 0, "V")
             w_evac(0, 1, "S")
             s_add(1, 0, 1)
             w_quant(1, 1, 0)
@@ -298,12 +320,13 @@ def tile_af_2_pa_t_kernel(tc, t, W1, b1, g1, beta1, m1, v1, W2, b2, g2, beta2, m
             s_add(1, 2, 1)
             s_add(1, 3, 1)
             s_tr(1, 1)
+            params_cast(1)
             params_tr(1)
             rg(0)
             mm1(0, 1, None, (2, 3))
-            relu(0, 1, None, (0, 1))
+            relu(0, 1, None, (0,))
             s_evac(1, 1, "SS")
-            relu(0, 1, None, (2, 3))
+            relu(0, 1, None, (1, 2, 3))
             s_quant(1)
             s_add(2, 0, 2)
             q2(0)

@@ -49,7 +49,6 @@ def tile_af_2_pa_t_kernel(tc, t, W1, b1, g1, beta1, m1, v1, W2, b2, g2, beta2, m
         xv2 = const.tile([16, P], F32, name="xv2")
         xf1 = const.tile([P, 2, P], F32, name="xf1")
         xf2 = const.tile([P, P], F32, name="xf2")
-        zb = const.tile([P, CH], BF16, name="zb")
         dummy = const.tile([P, 1], F32, name="dummy")
         pr = [const.tile([P, 5, 8], F32, name="pr1"), const.tile([P, 5, 16], F32, name="pr2")]
         sc = [const.tile([P, 8], F32, name="sc1"), const.tile([P, 16], F32, name="sc2")]
@@ -62,14 +61,14 @@ def tile_af_2_pa_t_kernel(tc, t, W1, b1, g1, beta1, m1, v1, W2, b2, g2, beta2, m
         def load_t(c, bt0, nbt):
             nc.sync.dma_start(out=t_sb[c][:, bt0:bt0 + nbt], in_=t_v[:, c * BT + bt0:c * BT + bt0 + nbt])
 
-        def load_params(stage, which):
+        def load_params(queue, stage, which):
             vecs = ((v1, b1, g1, beta1, m1), (v2, b2, g2, beta2, m2))[stage]
             for v in which:
                 vec = vecs[v]
                 if stage == 0:
-                    nc.sync.dma_start(out=v1r[:] if v == 0 else x1[4 * v:4 * v + 4, :], in_=vec.rearrange("n (u c) -> (n u) c", c=256))
+                    queue.dma_start(out=v1r[:] if v == 0 else x1[4 * v:4 * v + 4, :], in_=vec.rearrange("n (u c) -> (n u) c", c=256))
                 else:
-                    nc.sync.dma_start(out=v2r[:] if v == 0 else x2[16 * v:16 * v + 16, :], in_=vec.rearrange("n (k c) -> (n k) c", c=P))
+                    queue.dma_start(out=v2r[:] if v == 0 else x2[16 * v:16 * v + 16, :], in_=vec.rearrange("n (k c) -> (n k) c", c=P))
 
         def params_sqrt(stage):
             x, xv = ((v1r.rearrange("r (p e) -> r e p", e=2), xv1), (v2r, xv2))[stage]
@@ -235,22 +234,16 @@ def tile_af_2_pa_t_kernel(tc, t, W1, b1, g1, beta1, m1, v1, W2, b2, g2, beta2, m
             def q2(j):
                 nc.vector.quantize_mx(out=hw[:, j, :].bitcast(FP8X4), scales=hs[:, j, :], in_=live[("hg", j)][:])
 
-            def warm(count):
-                acc = mp.tile([P, CH], F32, name="acc", tag="mp")
-                for i in range(count):
-                    nc.tensor.matmul(out=acc[:], lhsT=zb[:, 0:P], rhs=zb[:], start=True, stop=True)
-
-            nc.vector.memset(zb[:], 0.0)
             nc.vector.memset(x1[:], 0.0)
             nc.vector.memset(dummy[:], 0.0)
             nc.vector.memset(x2[:], 0.0)
+            load_params(nc.scalar, 0, (0,))
+            load_params(nc.scalar, 1, (0,))
+            load_params(nc.scalar, 0, (1, 2, 3, 4))
             nc.scalar.sqrt(out=dummy[:], in_=dummy[:])
             make_identity(nc, ident[:])
             load_w1(0, slice(0, 1))
-            load_params(0, (0,))
-            load_params(1, (0,))
             load_t(0, 0, 1)
-            load_params(0, (1, 2, 3, 4))
             load_t(0, 1, 1)
             load_w1(0, slice(1, 2))
             load_t(0, 2, 1)
@@ -258,34 +251,30 @@ def tile_af_2_pa_t_kernel(tc, t, W1, b1, g1, beta1, m1, v1, W2, b2, g2, beta2, m
             load_w1(1, slice(0, 2))
             for bt in range(BT):
                 load_t(1, bt, 1)
-            load_params(1, (1, 2, 3, 4))
+            load_params(nc.sync, 1, (1, 2, 3, 4))
             load_t(2, 0, 2)
             load_t(2, 2, 2)
             load_w2(0)
             load_t(3, 0, 2)
             load_t(3, 2, 2)
-            warm(5)
-            w_tr(1, 0, 0, 0)
-            w_tr(1, 0, 1, 0)
-            warm(3)
-            w_evac(0, 0, "S")
-            w_evac(1, 0, "S")
             params_sqrt(0)
             params_sqrt(1)
             nc.scalar.activation(out=dummy[:], in_=dummy[:], func=ACT.Sigmoid)
+            params_cast(0)
+            w_tr(1, 0, 0, 0)
+            w_tr(1, 0, 1, 0)
+            params_tr(0)
+            w_evac(0, 0, "S")
+            w_evac(1, 0, "S")
             s_add(0, 0, 1)
+            params_out(0)
             w_quant(1, 0, 0, 0)
             w_quant(1, 0, 1, 0)
-            params_cast(0)
-            params_tr(0)
-            warm(2)
             s_add(0, 1, 1)
-            params_out(0)
             s_tr(0, 0)
             s_evac(0, 0, "SS")
             w_tr(1, 0, 0, 1)
             w_tr(1, 0, 1, 1)
-            warm(3)
             load_w2(1)
             w_evac(0, 1, "S")
             w_evac(1, 1, "S")

@@ -180,12 +180,12 @@ def tile_af_2_pa_t_kernel(tc, t, W1, b1, g1, beta1, m1, v1, W2, b2, g2, beta2, m
 
             def s_tr(c, half):
                 for g in range(2):
-                    bank = tp.tile([P, 2, 256], F32, name="tpb", tag="tp")
-                    for x in range(2):
-                        words = live[("s", c)][:, 2 * half + x, :].bitcast(F32)
+                    live[("tbank", c, g, half)] = tp.tile([P, 2, 256], F32, name="tpb", tag="tp")
+                for x in range(2):
+                    words = live[("s", c)][:, 2 * half + x, :].bitcast(F32)
+                    for g in range(2):
                         for u in range(2):
-                            nc.tensor.transpose(bank[:, u, x * P:(x + 1) * P], words[:, 256 * g + u * P:256 * g + (u + 1) * P], ident[:])
-                    live[("tbank", c, g, half)] = bank
+                            nc.tensor.transpose(live[("tbank", c, g, half)][:, u, x * P:(x + 1) * P], words[:, 256 * g + u * P:256 * g + (u + 1) * P], ident[:])
 
             def s_evac(c, half, engs):
                 for g in range(2):
@@ -237,10 +237,10 @@ def tile_af_2_pa_t_kernel(tc, t, W1, b1, g1, beta1, m1, v1, W2, b2, g2, beta2, m
             nc.vector.memset(x1[:], 0.0)
             nc.vector.memset(dummy[:], 0.0)
             nc.vector.memset(x2[:], 0.0)
+            nc.scalar.sqrt(out=dummy[:], in_=dummy[:])
             load_params(nc.scalar, 0, (0,))
             load_params(nc.scalar, 1, (0,))
             load_params(nc.scalar, 0, (1, 2, 3, 4))
-            nc.scalar.sqrt(out=dummy[:], in_=dummy[:])
             make_identity(nc, ident[:])
             load_w1(0, slice(0, 1))
             load_t(0, 0, 1)
@@ -257,28 +257,28 @@ def tile_af_2_pa_t_kernel(tc, t, W1, b1, g1, beta1, m1, v1, W2, b2, g2, beta2, m
             load_w2(0)
             load_t(3, 0, 2)
             load_t(3, 2, 2)
+            w_tr(1, 0, 0, 0)
+            w_tr(1, 0, 1, 0)
+            w_evac(0, 0, "S")
+            w_evac(1, 0, "S")
+            s_add(0, 0, 1)
             params_sqrt(0)
             params_sqrt(1)
             nc.scalar.activation(out=dummy[:], in_=dummy[:], func=ACT.Sigmoid)
             params_cast(0)
-            w_tr(1, 0, 0, 0)
-            w_tr(1, 0, 1, 0)
-            params_tr(0)
-            w_evac(0, 0, "S")
-            w_evac(1, 0, "S")
-            s_add(0, 0, 1)
-            params_out(0)
             w_quant(1, 0, 0, 0)
             w_quant(1, 0, 1, 0)
             s_add(0, 1, 1)
             s_tr(0, 0)
+            params_tr(0)
             s_evac(0, 0, "SS")
+            s_add(0, 2, 1)
+            params_out(0)
             w_tr(1, 0, 0, 1)
             w_tr(1, 0, 1, 1)
             load_w2(1)
             w_evac(0, 1, "S")
             w_evac(1, 1, "S")
-            s_add(0, 2, 1)
             s_quant(0, 0)
             s_add(0, 3, 1)
             w_quant(1, 0, 0, 1)
@@ -319,6 +319,7 @@ def tile_af_2_pa_t_kernel(tc, t, W1, b1, g1, beta1, m1, v1, W2, b2, g2, beta2, m
             s_quant(1)
             s_add(2, 0, 2)
             q2(0)
+            s_add(2, 2, 2)
             params_out(1)
             for c in range(1, NCH):
                 mm1(c, 0)
@@ -326,19 +327,20 @@ def tile_af_2_pa_t_kernel(tc, t, W1, b1, g1, beta1, m1, v1, W2, b2, g2, beta2, m
                 if c < NCH - 1:
                     if c > 1:
                         s_add(c + 1, 0, 2)
+                        s_add(c + 1, 2, 2)
+                        q2(2 * c - 2)
                     rg(2 * c - 1)
-                    s_add(c + 1, 2, 2)
                     s_tr(c + 1, 0)
                     s_evac(c + 1, 0, "SS")
                     s_tr(c + 1, 1)
                     s_evac(c + 1, 1, "SS")
                     q2(2 * c - 1)
-                    rg(2 * c)
                     s_quant(c + 1)
-                    q2(2 * c)
+                    rg(2 * c)
                     mm1(c, 1)
                     relu(c, 1)
                 else:
+                    q2(2 * c - 2)
                     rg(2 * c - 1)
                     for n in range(NB):
                         for a in range(2):
@@ -347,9 +349,9 @@ def tile_af_2_pa_t_kernel(tc, t, W1, b1, g1, beta1, m1, v1, W2, b2, g2, beta2, m
                         for a in range(2):
                             for b in range(2):
                                 w_evac(a, b, "V" if b == 1 else "S")
-                        q2(2 * c - 1 + n)
                         w_quant(2, n, 0)
                         w_quant(2, n, 1)
+                        q2(2 * c - 1 + n)
                         rg(2 * c + n)
                         if n == 0:
                             mm1(c, 1)

@@ -61,14 +61,14 @@ def tile_af_2_pa_t_kernel(tc, t, W1, b1, g1, beta1, m1, v1, W2, b2, g2, beta2, m
         def load_t(c, bt0, nbt):
             nc.sync.dma_start(out=t_sb[c][:, bt0:bt0 + nbt], in_=t_v[:, c * BT + bt0:c * BT + bt0 + nbt])
 
-        def load_params(queue, stage, which):
+        def load_params(stage, which):
             vecs = ((v1, b1, g1, beta1, m1), (v2, b2, g2, beta2, m2))[stage]
             for v in which:
                 vec = vecs[v]
                 if stage == 0:
-                    queue.dma_start(out=v1r[:] if v == 0 else x1[4 * v:4 * v + 4, :], in_=vec.rearrange("n (u c) -> (n u) c", c=256))
+                    nc.sync.dma_start(out=v1r[:] if v == 0 else x1[4 * v:4 * v + 4, :], in_=vec.rearrange("n (u c) -> (n u) c", c=256))
                 else:
-                    queue.dma_start(out=v2r[:] if v == 0 else x2[16 * v:16 * v + 16, :], in_=vec.rearrange("n (k c) -> (n k) c", c=P))
+                    nc.sync.dma_start(out=v2r[:] if v == 0 else x2[16 * v:16 * v + 16, :], in_=vec.rearrange("n (k c) -> (n k) c", c=P))
 
         def params_sqrt(stage):
             x, xv = ((v1r.rearrange("r (p e) -> r e p", e=2), xv1), (v2r, xv2))[stage]
@@ -238,20 +238,20 @@ def tile_af_2_pa_t_kernel(tc, t, W1, b1, g1, beta1, m1, v1, W2, b2, g2, beta2, m
             nc.vector.memset(dummy[:], 0.0)
             nc.vector.memset(x2[:], 0.0)
             nc.scalar.sqrt(out=dummy[:], in_=dummy[:])
-            load_params(nc.scalar, 0, (0,))
-            load_params(nc.scalar, 1, (0,))
-            load_params(nc.scalar, 0, (1, 2, 3, 4))
             make_identity(nc, ident[:])
             load_w1(0, slice(0, 1))
             load_t(0, 0, 1)
+            load_params(0, (0,))
+            load_params(1, (0,))
             load_t(0, 1, 1)
             load_w1(0, slice(1, 2))
+            load_params(0, (1, 2, 3, 4))
             load_t(0, 2, 1)
             load_t(0, 3, 1)
             load_w1(1, slice(0, 2))
             for bt in range(BT):
                 load_t(1, bt, 1)
-            load_params(nc.sync, 1, (1, 2, 3, 4))
+            load_params(1, (1, 2, 3, 4))
             load_t(2, 0, 2)
             load_t(2, 2, 2)
             load_w2(0)

from contextlib import ExitStack

import concourse.mybir as mybir
from concourse.masks import make_identity

F32 = mybir.dt.float32
BF16 = mybir.dt.bfloat16
U32 = mybir.dt.uint32
U8 = mybir.dt.uint8
FP8X4 = mybir.dt.float8_e4m3fn_x4
ALU = mybir.AluOpType
ACT = mybir.ActivationFunctionType

P = 128
B, NB, DIM, INTER = 2048, 2, 1024, 512
EPS = 1e-5
CH = 512
NCH = B // CH
BT = CH // P
LAG = 2
FLOPS = 2 * B * DIM * NB * INTER * 2


def tile_af_2_pa_t_kernel(tc, t, W1, b1, g1, beta1, m1, v1, W2, b2, g2, beta2, m2, v2, out):
    nc = tc.nc
    with ExitStack() as ctx:
        ctx.enter_context(tc.manual_schedule())
        const = ctx.enter_context(tc.tile_pool(name="const", bufs=1))
        wtp = ctx.enter_context(tc.tile_pool(name="wtp", bufs=12))
        tp = ctx.enter_context(tc.psum_pool(name="tp", bufs=4))
        mp = ctx.enter_context(tc.psum_pool(name="mp", bufs=4))

        t_v = t.rearrange("(p k) n d -> p k n d", k=NCH * BT)
        out_v = out.rearrange("(p k) d -> p k d", k=NCH * BT)

        ident = const.tile([P, P], F32, name="ident")
        w1w = const.tile([P, 2, NB * INTER], U32, name="w1w", align_bytes=64)
        w1s = const.tile([P, 2, NB * INTER], U8, name="w1s", align_bytes=64)
        w2w = const.tile([P, NB, DIM], U32, name="w2w", align_bytes=64)
        w2s = const.tile([P, NB, DIM], U8, name="w2s", align_bytes=64)
        hw = const.tile([P, NCH * NB, CH], U32, name="hw", align_bytes=64)
        hs = const.tile([P, NCH * NB, CH], U8, name="hs", align_bytes=64)
        t_sb = [const.tile([P, BT, NB, DIM], BF16, name="t_sb%d" % c) for c in range(NCH)]
        x1 = const.tile([P, 256], BF16, name="x1")
        x2 = const.tile([P, P], BF16, name="x2")
        v1r = const.tile([4, 256], BF16, name="v1r")
        v2r = const.tile([16, P], BF16, name="v2r")
        xv1 = const.tile([4, 2, P], F32, name="xv1")
        xv2 = const.tile([16, P], F32, name="xv2")
        xf1 = const.tile([P, 2, P], F32, name="xf1")
        xf2 = const.tile([P, P], F32, name="xf2")
        dummy = const.tile([P, 1], F32, name="dummy")
        pr = [const.tile([P, 5, 8], F32, name="pr1"), const.tile([P, 5, 16], F32, name="pr2")]
        sc = [const.tile([P, 8], F32, name="sc1"), const.tile([P, 16], F32, name="sc2")]
        bi = [const.tile([P, 8], F32, name="bi1"), const.tile([P, 16], F32, name="bi2")]
        rs = [const.tile([P, 8], F32, name="rs1"), const.tile([P, 16], F32, name="rs2")]
        df = [const.tile([P, 8], F32, name="df1"), const.tile([P, 16], F32, name="df2")]

        live = {}

        def load_t(c, bt0, nbt):
            nc.sync.dma_start(out=t_sb[c][:, bt0:bt0 + nbt], in_=t_v[:, c * BT + bt0:c * BT + bt0 + nbt])

        def load_params(stage, which):
            vecs = ((v1, b1, g1, beta1, m1), (v2, b2, g2, beta2, m2))[stage]
            for v in which:
                vec = vecs[v]
                if stage == 0:
                    nc.sync.dma_start(out=v1r[:] if v == 0 else x1[4 * v:4 * v + 4, :], in_=vec.rearrange("n (u c) -> (n u) c", c=256))
                else:
                    nc.sync.dma_start(out=v2r[:] if v == 0 else x2[16 * v:16 * v + 16, :], in_=vec.rearrange("n (k c) -> (n k) c", c=P))

        def params_sqrt(stage):
            x, xv = ((v1r.rearrange("r (p e) -> r e p", e=2), xv1), (v2r, xv2))[stage]
            nc.vector.tensor_scalar(out=xv[:], in0=x[:], scalar1=1.0, scalar2=EPS, op0=ALU.mult, op1=ALU.add)
            nc.scalar.sqrt(out=xv[:], in_=xv[:])

        def params_cast(stage):
            x, xf, xv, nv = ((x1.rearrange("r (p e) -> r e p", e=2), xf1, xv1, 4), (x2, xf2, xv2, 16))[stage]
            nc.gpsimd.tensor_scalar(out=xf[:], in0=x[:], scalar1=1.0, scalar2=0.0, op0=ALU.mult, op1=ALU.add)
            nc.gpsimd.tensor_scalar(out=xf[0:nv], in0=xv[:], scalar1=1.0, scalar2=0.0, op0=ALU.mult, op1=ALU.add)

        def params_tr(stage):
            bank = tp.tile([P, 2, P], F32, name="tpb", tag="tp")
            if stage == 0:
                for e in range(2):
                    nc.tensor.transpose(bank[:, e, :], xf1[:, e, :], ident[:])
            else:
                nc.tensor.transpose(bank[:, 0, :], xf2[:], ident[:])
            live["pbank"] = bank

        def params_out(stage):
            bank = live["pbank"]
            if stage == 0:
                nc.vector.tensor_copy(out=pr[0].rearrange("p v (e j) -> p v e j", e=2), in_=bank[:, :, 0:20].rearrange("p e (v j) -> p v e j", v=5))
            else:
                nc.vector.tensor_copy(out=pr[1][:], in_=bank[:, 0, 0:80].rearrange("p (v j) -> p v j", v=5))
            q = pr[stage]
            nc.vector.reciprocal(out=rs[stage][:], in_=q[:, 0, :])
            nc.gpsimd.tensor_tensor(out=df[stage][:], in0=q[:, 1, :], in1=q[:, 4, :], op=ALU.subtract)
            nc.gpsimd.tensor_tensor(out=sc[stage][:], in0=q[:, 2, :], in1=rs[stage][:], op=ALU.mult)
            nc.gpsimd.tensor_tensor(out=df[stage][:], in0=df[stage][:], in1=sc[stage][:], op=ALU.mult)
            nc.gpsimd.tensor_tensor(out=bi[stage][:], in0=df[stage][:], in1=q[:, 3, :], op=ALU.add)

        def mm2(c, n, dg):
            for kk in range(4):
                acc = mp.tile([P, CH], F32, name="acc", tag="mp")
                cols = slice((4 * dg + kk) * P, (4 * dg + kk + 1) * P)
                nc.tensor.matmul_mx(out=acc[:], lhsT=w2w[:, n, cols].bitcast(FP8X4), lhsT_scale=w2s[:, n, cols],
                                    rhs=hw[:, 2 * c + n, :].bitcast(FP8X4), rhs_scale=hs[:, 2 * c + n, :], start=True, stop=True)
                live[("acc2", kk)] = acc

        def sig(c, n, dg):
            for kk in range(4):
                wT = wtp.tile([P, CH], F32, name="wT")
                col = 8 * n + 4 * dg + kk
                nc.scalar.activation(out=wT[:], in_=live[("acc2", kk)][:], func=ACT.Sigmoid,
                                     bias=bi[1][:, col:col + 1], scale=sc[1][:, col:col + 1])
                live[("wT", c, n, dg, kk)] = wT

        units = [(c, n, dg) for c in range(NCH) for dg in range(2) for n in range(NB)]

        with ExitStack() as ph1:
            rawp = ph1.enter_context(tc.tile_pool(name="rawp", bufs=3))
            wgrpp = ph1.enter_context(tc.tile_pool(name="wgrpp", bufs=4))
            ssp = ph1.enter_context(tc.tile_pool(name="ssp", bufs=2))
            sgp = ph1.enter_context(tc.tile_pool(name="sgp", bufs=3))
            swp = ph1.enter_context(tc.tile_pool(name="swp", bufs=2))
            hp = ph1.enter_context(tc.tile_pool(name="hp", bufs=3))

            def load_w1(n, halves):
                if ("w1raw", n) not in live:
                    live[("w1raw", n)] = rawp.tile([P, 4096], BF16, name="wraw")
                src = W1[n].rearrange("(u p e) d -> p u (e d)", u=2, p=P, e=2)
                dst = live[("w1raw", n)].rearrange("p (u x) -> p u x", u=2)
                nc.sync.dma_start(out=dst[:, halves], in_=src[:, halves])

            def load_w2(n):
                raw = rawp.tile([P, 4096], BF16, name="wraw")
                nc.sync.dma_start(out=raw.rearrange("p (k i) -> p k i", k=8), in_=W2[n].rearrange("(k p) i -> p k i", p=P))
                live[("w2raw", n)] = raw

            def w_tr(kind, n, a, b):
                bank = tp.tile([P, 2, 256], F32, name="tpb", tag="tp")
                for x in range(2):
                    if kind == 1:
                        words = live[("w1raw", n)][:, b * 2048 + x * 1024:b * 2048 + (x + 1) * 1024].bitcast(F32)[:, 256 * a:256 * a + 256]
                    else:
                        k = 4 * a + 2 * b + x
                        words = live[("w2raw", n)][:, k * 512:(k + 1) * 512].bitcast(F32)
                    for u in range(2):
                        nc.tensor.transpose(bank[:, u, x * P:(x + 1) * P], words[:, u * P:(u + 1) * P], ident[:])
                live[("wbank", a, b)] = bank

            def w_evac(a, b, eng):
                if b == 0:
                    live[("wgrp", a)] = wgrpp.tile([P, 2048], BF16, name="wgrp", align_bytes=64)
                dst = live[("wgrp", a)].bitcast(F32).rearrange("p (c u) -> p c u", u=2)[:, b * 256:(b + 1) * 256, :]
                src = live[("wbank", a, b)].rearrange("p u c -> p c u")
                if eng == "S":
                    nc.scalar.copy(out=dst, in_=src)
                else:
                    nc.vector.tensor_copy(out=dst, in_=src)

            def w_quant(kind, n, a, b=None):
                grp = live[("wgrp", a)]
                lo, hi = (0, 512) if b is None else (256 * b, 256 * b + 256)
                if kind == 1:
                    cols = slice(n * 512 + lo, n * 512 + hi)
                    nc.vector.quantize_mx(out=w1w[:, a, cols].bitcast(FP8X4), scales=w1s[:, a, cols], in_=grp[:, 4 * lo:4 * hi])
                else:
                    cols = slice(a * 512 + lo, a * 512 + hi)
                    nc.vector.quantize_mx(out=w2w[:, n, cols].bitcast(FP8X4), scales=w2s[:, n, cols], in_=grp[:, 4 * lo:4 * hi])

            def s_add(c, bt0, nbt):
                if bt0 == 0:
                    live[("s", c)] = ssp.tile([P, BT, DIM], BF16, name="s_sb")
                rows = slice(bt0, bt0 + nbt)
                nc.vector.tensor_tensor(out=live[("s", c)][:, rows, :], in0=t_sb[c][:, rows, 0, :], in1=t_sb[c][:, rows, 1, :], op=ALU.add)

            def s_tr(c, half):
                for g in range(2):
                    live[("tbank", c, g, half)] = tp.tile([P, 2, 256], F32, name="tpb", tag="tp")
                for x in range(2):
                    words = live[("s", c)][:, 2 * half + x, :].bitcast(F32)
                    for g in range(2):
                        for u in range(2):
                            nc.tensor.transpose(live[("tbank", c, g, half)][:, u, x * P:(x + 1) * P], words[:, 256 * g + u * P:256 * g + (u + 1) * P], ident[:])

            def s_evac(c, half, engs):
                for g in range(2):
                    if ("sg", c, g) not in live:
                        live[("sg", c, g)] = sgp.tile([P, 2048], BF16, name="sg", align_bytes=64)
                    dst = live[("sg", c, g)].bitcast(F32).rearrange("p (b u) -> p b u", u=2)[:, half * 256:(half + 1) * 256, :]
                    src = live[("tbank", c, g, half)].rearrange("p u b -> p b u")
                    if engs[g] == "S":
                        nc.scalar.copy(out=dst, in_=src)
                    else:
                        nc.vector.tensor_copy(out=dst, in_=src)

            def s_quant(c, half=None):
                if ("sw", c) not in live:
                    live[("sw", c)] = swp.tile([P, 2, CH], U32, name="sw", align_bytes=64)
                    live[("ss", c)] = swp.tile([P, 2, CH], U8, name="ss", align_bytes=64)
                lo, hi = (0, 512) if half is None else (256 * half, 256 * half + 256)
                for g in range(2):
                    nc.vector.quantize_mx(out=live[("sw", c)][:, g, lo:hi].bitcast(FP8X4), scales=live[("ss", c)][:, g, lo:hi], in_=live[("sg", c, g)][:, 4 * lo:4 * hi])

            def mm1(c, n, half=None, tts=(0, 1, 2, 3)):
                lo, hi = (0, 512) if half is None else (256 * half, 256 * half + 256)
                for tt in tts:
                    acc = mp.tile([P, hi - lo], F32, name="acc", tag="mp")
                    cols = slice(n * 512 + tt * P, n * 512 + (tt + 1) * P)
                    for g in range(2):
                        nc.tensor.matmul_mx(out=acc[:], lhsT=w1w[:, g, cols].bitcast(FP8X4), lhsT_scale=w1s[:, g, cols],
                                            rhs=live[("sw", c)][:, g, lo:hi].bitcast(FP8X4), rhs_scale=live[("ss", c)][:, g, lo:hi],
                                            start=(g == 0), stop=(g == 1))
                    live[("acc1", tt)] = acc

            def relu(c, n, half=None, tts=(0, 1, 2, 3)):
                lo, hi = (0, 512) if half is None else (256 * half, 256 * half + 256)
                if ("hT", c, n) not in live:
                    live[("hT", c, n)] = hp.tile([P, 4, CH], BF16, name="hT")
                for tt in tts:
                    col = (tt % 2) * 4 + 2 * n + tt // 2
                    nc.scalar.activation(out=live[("hT", c, n)][:, tt, lo:hi], in_=live[("acc1", tt)][:], func=ACT.Relu,
                                         bias=bi[0][:, col:col + 1], scale=sc[0][:, col:col + 1])

            def rg(j):
                hg = hp.tile([P, 4 * CH], BF16, name="hg", align_bytes=64)
                nc.vector.tensor_copy(out=hg.rearrange("p (c i t) -> p c t i", i=4, t=4), in_=live[("hT", j // 2, j % 2)].rearrange("p t (c i) -> p c t i", i=4))
                live[("hg", j)] = hg

            def q2(j):
                nc.vector.quantize_mx(out=hw[:, j, :].bitcast(FP8X4), scales=hs[:, j, :], in_=live[("hg", j)][:])

            nc.vector.memset(x1[:], 0.0)
            nc.vector.memset(dummy[:], 0.0)
            nc.vector.memset(x2[:], 0.0)
            nc.scalar.sqrt(out=dummy[:], in_=dummy[:])
            make_identity(nc, ident[:])
            load_w1(0, slice(0, 1))
            load_t(0, 0, 1)
            load_params(0, (0,))
            load_params(1, (0,))
            load_t(0, 1, 1)
            load_w1(0, slice(1, 2))
            load_params(0, (1, 2, 3, 4))
            load_t(0, 2, 1)
            load_t(0, 3, 1)
            load_w1(1, slice(0, 2))
            for bt in range(BT):
                load_t(1, bt, 1)
            load_params(1, (1, 2, 3, 4))
            load_t(2, 0, 2)
            load_t(2, 2, 2)
            load_w2(0)
            load_t(3, 0, 2)
            load_t(3, 2, 2)
            w_tr(1, 0, 0, 0)
            w_tr(1, 0, 1, 0)
            w_evac(0, 0, "S")
            w_evac(1, 0, "S")
            s_add(0, 0, 1)
            params_sqrt(0)
            params_sqrt(1)
            nc.scalar.activation(out=dummy[:], in_=dummy[:], func=ACT.Sigmoid)
            params_cast(0)
            w_quant(1, 0, 0, 0)
            w_quant(1, 0, 1, 0)
            s_add(0, 1, 1)
            s_tr(0, 0)
            params_tr(0)
            s_evac(0, 0, "SS")
            s_add(0, 2, 1)
            params_out(0)
            w_tr(1, 0, 0, 1)
            w_tr(1, 0, 1, 1)
            load_w2(1)
            w_evac(0, 1, "S")
            w_evac(1, 1, "S")
            s_quant(0, 0)
            s_add(0, 3, 1)
            w_quant(1, 0, 0, 1)
            w_quant(1, 0, 1, 1)
            mm1(0, 0, 0, (0, 1))
            s_tr(0, 1)
            mm1(0, 0, 0, (2, 3))
            relu(0, 0, 0, (0, 1))
            s_evac(0, 1, "VS")
            relu(0, 0, 0, (2, 3))
            s_quant(0, 1)
            for a in range(2):
                for b in range(2):
                    w_tr(1, 1, a, b)
            mm1(0, 0, 1)
            w_evac(0, 0, "V")
            w_evac(0, 1, "S")
            s_add(1, 0, 1)
            w_quant(1, 1, 0)
            w_evac(1, 0, "S")
            w_evac(1, 1, "S")
            s_add(1, 1, 1)
            w_quant(1, 1, 1)
            relu(0, 0, 1)
            s_tr(1, 0)
            mm1(0, 1, None, (0, 1))
            s_evac(1, 0, "SS")
            s_add(1, 2, 1)
            s_add(1, 3, 1)
            s_tr(1, 1)
            params_cast(1)
            params_tr(1)
            rg(0)
            mm1(0, 1, None, (2, 3))
            relu(0, 1, None, (0,))
            s_evac(1, 1, "SS")
            relu(0, 1, None, (1, 2, 3))
            s_quant(1)
            s_add(2, 0, 2)
            q2(0)
            s_add(2, 2, 2)
            params_out(1)
            for c in range(1, NCH):
                mm1(c, 0)
                relu(c, 0)
                if c < NCH - 1:
                    if c > 1:
                        s_add(c + 1, 0, 2)
                        s_add(c + 1, 2, 2)
                        q2(2 * c - 2)
                    rg(2 * c - 1)
                    s_tr(c + 1, 0)
                    s_evac(c + 1, 0, "SS")
                    s_tr(c + 1, 1)
                    s_evac(c + 1, 1, "SS")
                    q2(2 * c - 1)
                    s_quant(c + 1)
                    rg(2 * c)
                    mm1(c, 1)
                    relu(c, 1)
                else:
                    q2(2 * c - 2)
                    rg(2 * c - 1)
                    for n in range(NB):
                        for a in range(2):
                            for b in range(2):
                                w_tr(2, n, a, b)
                        for a in range(2):
                            for b in range(2):
                                w_evac(a, b, "V" if b == 1 else "S")
                        w_quant(2, n, 0)
                        w_quant(2, n, 1)
                        q2(2 * c - 1 + n)
                        rg(2 * c + n)
                        if n == 0:
                            mm1(c, 1)
                            relu(c, 1)
                    for n in range(NB):
                        mm2(*units[n])
                        sig(*units[n])
            q2(7)

        with ExitStack() as ph2:
            op = ph2.enter_context(tc.tile_pool(name="op", bufs=3))
            pp = ph2.enter_context(tc.tile_pool(name="pp", bufs=2))

            def t2(c, n, dg):
                for bt in range(BT):
                    bank = tp.tile([P, CH], F32, name="tpb", tag="tp")
                    for kk in range(4):
                        nc.tensor.transpose(bank[:, kk * P:(kk + 1) * P], live[("wT", c, n, dg, kk)][:, bt * P:(bt + 1) * P], ident[:])
                    live[("wps", bt)] = bank

            def prod(c, n, dg, bt):
                if bt == 0:
                    if n == 0:
                        live["o"] = op.tile([P, BT, CH], F32, name="o")
                    else:
                        live["p1"] = pp.tile([P, BT, CH], F32, name="p1")
                dst = live["o"] if n == 0 else live["p1"]
                nc.vector.scalar_tensor_tensor(out=dst[:, bt, :], in0=live[("wps", bt)][:], scalar=3.0,
                                               in1=t_sb[c][:, bt, n, dg * CH:(dg + 1) * CH], op0=ALU.mult, op1=ALU.mult)

            def add(bt, eng):
                o = live["o"]
                p1 = live["p1"]
                if eng == "G":
                    nc.gpsimd.tensor_tensor(out=o[:, bt, :], in0=o[:, bt, :], in1=p1[:, bt, :], op=ALU.add)
                else:
                    nc.vector.tensor_tensor(out=o[:, bt, :], in0=o[:, bt, :], in1=p1[:, bt, :], op=ALU.add)

            def store(c, dg, bt0, nbt):
                nc.sync.dma_start(out=out_v[:, c * BT + bt0:c * BT + bt0 + nbt, dg * CH:(dg + 1) * CH], in_=live["o"][:, bt0:bt0 + nbt, :])

            for k in range(LAG, len(units) + LAG):
                t2(*units[k - LAG])
                if k < len(units):
                    mm2(*units[k])
                    sig(*units[k])
                c, n, dg = units[k - LAG]
                last = k == len(units) + LAG - 1
                for bt in range(BT):
                    prod(c, n, dg, bt)
                    if last and bt < 2:
                        add(bt, "G")
                if last:
                    add(2, "V")
                    add(3, "V")
                    for bt in range(BT):
                        store(c, dg, bt, 1)
                if n == 1 and not last:
                    for bt in range(BT):
                        add(bt, "G")
                    store(c, dg, 0, BT)
